import numpy as np
import ml_dtypes


def mxq(x, axis, fmt="e4m3"):
    dtype, down = {"e4m3": (ml_dtypes.float8_e4m3fn, 7), "e5m2": (ml_dtypes.float8_e5m2, 14)}[fmt]
    v = np.moveaxis(np.asarray(x, np.float32).astype(ml_dtypes.bfloat16).astype(np.float64), axis, -1)
    blocks = v.reshape(v.shape[:-1] + (-1, 32))
    amax = np.abs(blocks).max(-1, keepdims=True)
    byte = np.maximum(np.where(amax > 0, np.frexp(amax)[1] - 1 + 127, 0) - down, 1)
    scale = np.exp2(byte - 127.0)
    codes = (blocks / scale).astype(np.float32).astype(dtype).astype(np.float64)
    return np.moveaxis((codes * scale).reshape(v.shape), -1, axis)


WIDE = False


def mx_kscale(k):
    if not WIDE:
        return np.ones(k)
    levels = np.array([10, -10, 5, -5, 0])
    a = np.random.permutation(np.resize(levels, k // 512 * 4)).reshape(k // 512, 4)
    idx = np.arange(k)
    return np.exp2(a[idx // 512, idx % 128 // 32])


BF16 = ml_dtypes.bfloat16


def bf(x):
    return np.asarray(x, np.float32).astype(BF16)


def f64(x):
    return np.asarray(x).astype(np.float64)


E2M1 = np.array([0.0, 0.5, 1.0, 1.5, 2.0, 3.0, 4.0, 6.0, -0.0, -0.5, -1.0, -1.5, -2.0, -3.0, -4.0, -6.0])


def pack_weight(w, fmt):
    k, n = w.shape
    w = f64(bf(w)).reshape(k // 32, 32, n)
    amax = np.abs(w).max(1)
    if fmt == "e4m3":
        byte = np.frexp(amax)[1] - 1 + 127 - 7
    else:
        mant, ex = np.frexp(amax / 6.0)
        byte = np.where(mant > 0.5, ex, ex - 1) + 127
    byte = np.clip(np.where(amax > 0, byte, 1), 1, 254)
    scaled = (w * np.exp2(127.0 - byte)[:, None, :]).reshape(k, n).astype(np.float32)
    by_word = np.ascontiguousarray(scaled.reshape(k // 512, 128, 4, n).transpose(0, 1, 3, 2))
    if fmt == "e4m3":
        words = by_word.astype(ml_dtypes.float8_e4m3fn).view(np.uint8)
    else:
        c = by_word.astype(ml_dtypes.float4_e2m1fn).view(np.uint8) & 0xF
        words = c[..., 0::2] | (c[..., 1::2] << 4)
    return np.ascontiguousarray(words), np.ascontiguousarray(byte.astype(np.uint8).reshape(k // 512, 16, n))


def unpack_weight(words, scales, fmt):
    g, p, n, _ = words.shape
    if fmt == "e4m3":
        vals = np.ascontiguousarray(words).view(ml_dtypes.float8_e4m3fn).astype(np.float64)
    else:
        nib = np.empty((g, p, n, 4), np.uint8)
        nib[..., 0::2] = words & 0xF
        nib[..., 1::2] = words >> 4
        vals = E2M1[nib]
    vals = vals * np.repeat(np.exp2(scales.astype(np.float64) - 127.0), 8, axis=1)[..., None]
    return vals.transpose(0, 1, 3, 2).reshape(g * 512, n)


B, N, NIN, CTX, H, NOUT = 2, 512, 512, 3, 1024, 2
F = NIN * CTX


def shift_down(y, d):
    return np.pad(y[:, :-d, :], ((0, 0), (d, 0), (0, 0)))


def shift_up(y, d):
    return np.pad(y[:, d:, :], ((0, 0), (0, d), (0, 0)))


def context_linear(xq, wt, shifts):
    y = xq @ wt[:NIN]
    c = 1
    for d in range(1, CTX // 2 + 1):
        for shift in shifts:
            y = y + shift(xq @ wt[c * NIN:(c + 1) * NIN], d)
            c += 1
    return y


def setup_inputs():
    s, u = mx_kscale(NIN), mx_kscale(H)
    x_l = bf(np.random.standard_normal((B, N, NIN)) * s)
    w_l = np.random.standard_normal((H, F)) / np.sqrt(F) / np.tile(s, CTX) * u[:, None]
    words, scales = pack_weight(np.ascontiguousarray(w_l.T), "e4m3")
    b_l = bf(np.random.standard_normal(H) * 0.3 * u)
    W_bil = bf(np.random.standard_normal((NOUT, H, H)) * 0.2 / np.sqrt(H) / u[None, :, None])
    return {"x_l": x_l, "W_l_words": words, "W_l_scales": scales, "b_l": b_l, "W_bil": W_bil}


def reference(x_l, W_l_words, W_l_scales, b_l, W_bil):
    xq = mxq(f64(x_l), 2, "e4m3")
    hl = np.maximum(context_linear(xq, unpack_weight(W_l_words, W_l_scales, "e4m3"), (shift_down, shift_up)) + f64(b_l), 0.0)
    wb = f64(W_bil).transpose(1, 0, 2).reshape(H, NOUT * H)
    t = mxq(hl, 2, "e4m3") @ mxq(wb, 0, "e4m3")
    return t.reshape(B, N, NOUT, H)

@@ -1,0 +1,194 @@
+from contextlib import ExitStack
+
+import concourse.mybir as mybir
+from concourse.masks import make_identity
+
+F32 = mybir.dt.float32
+BF16 = mybir.dt.bfloat16
+I32 = mybir.dt.int32
+U32 = mybir.dt.uint32
+U8 = mybir.dt.uint8
+FP8X4 = mybir.dt.float8_e4m3fn_x4
+RELU = mybir.ActivationFunctionType.Relu
+
+P = 128
+PACK = 4
+K_PASS = P * PACK
+BANK = 512
+
+SEQS = 2
+POS = 512
+FEAT = 512
+HID = 1024
+MAPS = 2
+TOKENS = SEQS * POS
+
+LANES = POS // P
+SLOTS = LANES + 2
+SHIFT_OF_GROUP = (0, -1, 1)
+H_TILES = HID // P
+H_PASSES = HID // K_PASS
+
+FLOPS = 2 * TOKENS * (3 * FEAT) * HID + 2 * TOKENS * HID * (MAPS * HID)
+
+
+def tile_bilinearpairedlayer_pa_kernel(tc, x_l, W_l_words, W_l_scales, b_l, W_bil, out):
+    nc = tc.nc
+    with ExitStack() as ctx:
+        keep = ctx.enter_context(tc.tile_pool(name="keep", bufs=1))
+        raw_pool = ctx.enter_context(tc.tile_pool(name="raw", bufs=MAPS * H_PASSES))
+        stage = ctx.enter_context(tc.tile_pool(name="stage", bufs=3))
+        out_pool = ctx.enter_context(tc.tile_pool(name="outs", bufs=6))
+        psum = ctx.enter_context(tc.psum_pool(name="psum", bufs=8))
+
+        ident = keep.tile([P, P], F32)
+        x_rows = keep.tile([P, SEQS, LANES * FEAT], BF16)
+        x_grouped = keep.tile([P, SEQS, SLOTS * P, PACK], BF16, align_bytes=64)
+        x_codes = keep.tile([P, SEQS, SLOTS * P], U32, align_bytes=64)
+        x_scales = keep.tile([P, SEQS, SLOTS * P], U8, align_bytes=64)
+        w_codes = keep.tile([P, 3, HID], U32, align_bytes=64)
+        w_scales = keep.tile([P, HID], U8, align_bytes=64)
+        bias_rows = keep.tile([P, P], BF16)
+        bias_rows_f32 = keep.tile([P, P], F32)
+        bias_cols = keep.tile([P, H_TILES], F32)
+        h_codes = keep.tile([P, H_PASSES, TOKENS], U32, align_bytes=64)
+        h_scales = keep.tile([P, H_PASSES, TOKENS], U8, align_bytes=64)
+        v_codes = keep.tile([P, H_PASSES, MAPS * HID], U32, align_bytes=64)
+        v_scales = keep.tile([P, H_PASSES, MAPS * HID], U8, align_bytes=64)
+
+        x_words = x_rows[:].bitcast(F32)
+        x_grouped_words = x_grouped[:].bitcast(F32)
+
+        nc.vector.memset(w_scales[:].bitcast(I32), 0)
+        nc.vector.memset(bias_rows[:], 0.0)
+        nc.vector.memset(x_grouped_words[:, :, 0, :], 0.0)
+        nc.vector.memset(x_grouped_words[:, :, SLOTS * P - 1, :], 0.0)
+        make_identity(nc, ident[:])
+
+        for quad in range(4):
+            nc.sync.dma_start(
+                out=w_scales[32 * quad : 32 * quad + 12, :].bitcast(I32),
+                in_=W_l_scales[:, 4 * quad : 4 * quad + 4, :].bitcast(I32),
+            )
+        nc.sync.dma_start(out=bias_rows[0:H_TILES, :], in_=b_l.rearrange("(j p) -> j p", p=P))
+        for b in range(SEQS):
+            nc.sync.dma_start(out=x_rows[:, b, :], in_=x_l[b].rearrange("(a r) k -> a (r k)", r=LANES))
+        for g in range(3):
+            nc.sync.dma_start(
+                out=w_codes[:, g, :].bitcast(I32),
+                in_=W_l_words[g].rearrange("p n t -> p (n t)").bitcast(I32),
+            )
+        v_raw = []
+        for m in range(MAPS):
+            by_pass = W_bil[m].rearrange("(c t p) n -> c p t n", t=PACK, p=P)
+            for c in range(H_PASSES):
+                raw = raw_pool.tile([P, PACK, HID], BF16, name="raw")
+                nc.sync.dma_start(out=raw[:], in_=by_pass[c])
+                v_raw.append(raw)
+
+        for b in range(SEQS):
+            for pair in range(LANES // 2):
+                flipped = psum.tile([P, 2, 2, P], F32, tag="bank", name="flipped")
+                for s in range(2):
+                    first = (2 * pair + s) * (FEAT // 2)
+                    for u in range(2):
+                        nc.tensor.transpose(
+                            out=flipped[:, s, u, :],
+                            in_=x_words[:, b, first + u : first + FEAT // 2 : 2],
+                            identity=ident[:],
+                        )
+                columns = slice((1 + 2 * pair) * P, (3 + 2 * pair) * P)
+                target = x_grouped_words[:, b, columns, :].rearrange("p (s a) u -> p s a u", s=2)
+                source = flipped[:].rearrange("p s u a -> p s a u")
+                if pair == 0:
+                    nc.vector.tensor_copy(out=target, in_=source)
+                else:
+                    nc.scalar.copy(out=target, in_=source)
+            nc.vector.tensor_copy(
+                out=x_grouped_words[:, b, 1:P, :], in_=x_grouped_words[:, b, LANES * P : (LANES + 1) * P - 1, :]
+            )
+            nc.vector.tensor_copy(
+                out=x_grouped_words[:, b, (LANES + 1) * P : SLOTS * P - 1, :],
+                in_=x_grouped_words[:, b, P + 1 : 2 * P, :],
+            )
+            for columns in (slice(P, (LANES + 1) * P), slice(0, P), slice((LANES + 1) * P, SLOTS * P)):
+                nc.vector.quantize_mx(
+                    out=x_codes[:, b, columns].bitcast(FP8X4),
+                    scales=x_scales[:, b, columns],
+                    in_=x_grouped[:, b, columns, :].rearrange("p c t -> p (c t)"),
+                )
+
+        nc.vector.tensor_copy(out=bias_rows_f32[:], in_=bias_rows[:])
+        bias_flipped = psum.tile([P, P], F32, tag="bank", name="bias_flipped")
+        nc.tensor.transpose(out=bias_flipped[:], in_=bias_rows_f32[:], identity=ident[:])
+        nc.vector.tensor_copy(out=bias_cols[:], in_=bias_flipped[:, 0:H_TILES])
+
+        def regroup(engine_copy, planes, name):
+            grouped = stage.tile([P, BANK, PACK], BF16, align_bytes=64, name=name)
+            engine_copy(
+                out=grouped[:].rearrange("p (c i) t -> p c t i", i=4),
+                in_=planes.rearrange("p t (c i) -> p c t i", i=4),
+            )
+            return grouped
+
+        def quantise(grouped, codes, scales):
+            nc.vector.quantize_mx(
+                out=codes.bitcast(FP8X4), scales=scales, in_=grouped[:].rearrange("p c t -> p (c t)")
+            )
+
+        for b in range(SEQS):
+            for c in range(H_PASSES):
+                h_planes = stage.tile([P, PACK, POS], BF16, name="h_planes")
+                for t in range(PACK):
+                    j = PACK * c + t
+                    units = slice(j * P, (j + 1) * P)
+                    pre = psum.tile([P, POS], F32, tag="bank", name="pre")
+                    for g in range(3):
+                        first = (1 + SHIFT_OF_GROUP[g]) * P
+                        nc.tensor.matmul_mx(
+                            out=pre[:],
+                            lhsT=w_codes[:, g, units].bitcast(FP8X4),
+                            lhsT_scale=w_scales[4 * g : P, units],
+                            rhs=x_codes[:, b, first : first + POS].bitcast(FP8X4),
+                            rhs_scale=x_scales[:, b, first : first + POS],
+                            start=(g == 0),
+                            stop=(g == 2),
+                        )
+                    nc.scalar.activation(out=h_planes[:, t, :], in_=pre[:], func=RELU, bias=bias_cols[:, j : j + 1], scale=1.0)
+
+                quarter = H_PASSES * b + c
+                v_map, v_pass = quarter // H_PASSES, quarter % H_PASSES
+                left = slice(v_map * HID, v_map * HID + BANK)
+                right = slice(v_map * HID + BANK, (v_map + 1) * HID)
+                v_left = regroup(nc.vector.tensor_copy, v_raw[quarter][:, :, 0:BANK], "v_left")
+                v_right = regroup(nc.scalar.copy, v_raw[quarter][:, :, BANK:HID], "v_right")
+                h_grouped = regroup(nc.vector.tensor_copy, h_planes[:], "h_grouped")
+                quantise(v_left, v_codes[:, v_pass, left], v_scales[:, v_pass, left])
+                tokens = slice(b * POS, (b + 1) * POS)
+                quantise(h_grouped, h_codes[:, c, tokens], h_scales[:, c, tokens])
+                quantise(v_right, v_codes[:, v_pass, right], v_scales[:, v_pass, right])
+
+        for m in range(MAPS):
+            for b in range(SEQS):
+                by_lane = out[b].rearrange("(a r) m g -> a r m g", r=LANES)
+                for r in range(LANES):
+                    tokens = slice(b * POS + r * P, b * POS + (r + 1) * P)
+                    result = out_pool.tile([P, HID], F32, name="result")
+                    for half in range(HID // BANK):
+                        columns = slice(m * HID + half * BANK, m * HID + (half + 1) * BANK)
+                        acc = psum.tile([P, BANK], F32, tag="bank", name="acc")
+                        for c in range(H_PASSES):
+                            nc.tensor.matmul_mx(
+                                out=acc[:],
+                                lhsT=h_codes[:, c, tokens].bitcast(FP8X4),
+                                lhsT_scale=h_scales[:, c, tokens],
+                                rhs=v_codes[:, c, columns].bitcast(FP8X4),
+                                rhs_scale=v_scales[:, c, columns],
+                                start=(c == 0),
+                                stop=(c == H_PASSES - 1),
+                            )
+                        if half == 0:
+                            nc.scalar.copy(out=result[:, 0:BANK], in_=acc[:])
+                        else:
+                            nc.vector.tensor_copy(out=result[:, BANK:HID], in_=acc[:])
+                    nc.sync.dma_start(out=by_lane[:, r, m, :], in_=result[:])

@@ -10,6 +10,7 @@ U32 = mybir.dt.uint32
 U8 = mybir.dt.uint8
 FP8X4 = mybir.dt.float8_e4m3fn_x4
 RELU = mybir.ActivationFunctionType.Relu
+IDENTITY = mybir.ActivationFunctionType.Identity
 
 P = 128
 PACK = 4
@@ -35,10 +36,11 @@ FLOPS = 2 * TOKENS * (3 * FEAT) * HID + 2 * TOKENS * HID * (MAPS * HID)
 def tile_bilinearpairedlayer_pa_kernel(tc, x_l, W_l_words, W_l_scales, b_l, W_bil, out):
     nc = tc.nc
     with ExitStack() as ctx:
+        ctx.enter_context(tc.manual_schedule())
         keep = ctx.enter_context(tc.tile_pool(name="keep", bufs=1))
         raw_pool = ctx.enter_context(tc.tile_pool(name="raw", bufs=MAPS * H_PASSES))
         stage = ctx.enter_context(tc.tile_pool(name="stage", bufs=3))
-        out_pool = ctx.enter_context(tc.tile_pool(name="outs", bufs=6))
+        out_pool = ctx.enter_context(tc.tile_pool(name="outs", bufs=8))
         psum = ctx.enter_context(tc.psum_pool(name="psum", bufs=8))
 
         ident = keep.tile([P, P], F32)
@@ -61,30 +63,33 @@ def tile_bilinearpairedlayer_pa_kernel(tc, x_l, W_l_words, W_l_scales, b_l, W_bi
 
         nc.vector.memset(w_scales[:].bitcast(I32), 0)
         nc.vector.memset(bias_rows[:], 0.0)
-        nc.vector.memset(x_grouped_words[:, :, 0, :], 0.0)
-        nc.vector.memset(x_grouped_words[:, :, SLOTS * P - 1, :], 0.0)
+        nc.vector.memset(x_grouped_words[:, :, 0:4, :], 0.0)
+        nc.vector.memset(x_grouped_words[:, :, SLOTS * P - 4 : SLOTS * P, :], 0.0)
         make_identity(nc, ident[:])
 
+        nc.scalar.dma_start(out=bias_rows[0:H_TILES, :], in_=b_l.rearrange("(j p) -> j p", p=P))
+        nc.sync.dma_start(out=x_rows[:, 0, :], in_=x_l[0].rearrange("(a r) k -> a (r k)", r=LANES))
         for quad in range(4):
             nc.sync.dma_start(
                 out=w_scales[32 * quad : 32 * quad + 12, :].bitcast(I32),
                 in_=W_l_scales[:, 4 * quad : 4 * quad + 4, :].bitcast(I32),
             )
-        nc.sync.dma_start(out=bias_rows[0:H_TILES, :], in_=b_l.rearrange("(j p) -> j p", p=P))
-        for b in range(SEQS):
-            nc.sync.dma_start(out=x_rows[:, b, :], in_=x_l[b].rearrange("(a r) k -> a (r k)", r=LANES))
-        for g in range(3):
-            nc.sync.dma_start(
-                out=w_codes[:, g, :].bitcast(I32),
-                in_=W_l_words[g].rearrange("p n t -> p (n t)").bitcast(I32),
-            )
+        nc.sync.dma_start(out=x_rows[:, 1, :], in_=x_l[1].rearrange("(a r) k -> a (r k)", r=LANES))
+        w_bytes = W_l_words.rearrange("g p n t -> p g (n t)")
         v_raw = []
         for m in range(MAPS):
             by_pass = W_bil[m].rearrange("(c t p) n -> c p t n", t=PACK, p=P)
             for c in range(H_PASSES):
+                if m == 0:
+                    nc.sync.dma_start(
+                        out=w_codes[:, :, c * K_PASS : (c + 1) * K_PASS].bitcast(I32),
+                        in_=w_bytes[:, :, c * K_PASS * PACK : (c + 1) * K_PASS * PACK].bitcast(I32),
+                    )
                 raw = raw_pool.tile([P, PACK, HID], BF16, name="raw")
                 nc.sync.dma_start(out=raw[:], in_=by_pass[c])
                 v_raw.append(raw)
+
+        nc.scalar.activation(out=bias_rows_f32[:], in_=bias_rows[:], func=IDENTITY)
 
         for b in range(SEQS):
             for pair in range(LANES // 2):
@@ -102,71 +107,89 @@ def tile_bilinearpairedlayer_pa_kernel(tc, x_l, W_l_words, W_l_scales, b_l, W_bi
                 source = flipped[:].rearrange("p s u a -> p s a u")
                 if pair == 0:
                     nc.vector.tensor_copy(out=target, in_=source)
+                    nc.vector.tensor_copy(
+                        out=x_grouped_words[:, b, (LANES + 1) * P : SLOTS * P - 1, :],
+                        in_=flipped[:, 0, :, 1:P].rearrange("p u a -> p a u"),
+                    )
                 else:
                     nc.scalar.copy(out=target, in_=source)
-            nc.vector.tensor_copy(
-                out=x_grouped_words[:, b, 1:P, :], in_=x_grouped_words[:, b, LANES * P : (LANES + 1) * P - 1, :]
-            )
-            nc.vector.tensor_copy(
-                out=x_grouped_words[:, b, (LANES + 1) * P : SLOTS * P - 1, :],
-                in_=x_grouped_words[:, b, P + 1 : 2 * P, :],
-            )
-            for columns in (slice(P, (LANES + 1) * P), slice(0, P), slice((LANES + 1) * P, SLOTS * P)):
+                    nc.scalar.copy(
+                        out=x_grouped_words[:, b, 1:P, :],
+                        in_=flipped[:, 1, :, 0 : P - 1].rearrange("p u a -> p a u"),
+                    )
+            for columns in (slice(0, LANES * P), slice(LANES * P, SLOTS * P)):
                 nc.vector.quantize_mx(
                     out=x_codes[:, b, columns].bitcast(FP8X4),
                     scales=x_scales[:, b, columns],
                     in_=x_grouped[:, b, columns, :].rearrange("p c t -> p (c t)"),
                 )
 
-        nc.vector.tensor_copy(out=bias_rows_f32[:], in_=bias_rows[:])
         bias_flipped = psum.tile([P, P], F32, tag="bank", name="bias_flipped")
         nc.tensor.transpose(out=bias_flipped[:], in_=bias_rows_f32[:], identity=ident[:])
-        nc.vector.tensor_copy(out=bias_cols[:], in_=bias_flipped[:, 0:H_TILES])
+        nc.scalar.copy(out=bias_cols[:], in_=bias_flipped[:, 0:H_TILES])
 
-        def regroup(engine_copy, planes, name):
+        def regroup(planes, name):
             grouped = stage.tile([P, BANK, PACK], BF16, align_bytes=64, name=name)
-            engine_copy(
+            nc.vector.tensor_copy(
                 out=grouped[:].rearrange("p (c i) t -> p c t i", i=4),
                 in_=planes.rearrange("p t (c i) -> p c t i", i=4),
             )
             return grouped
 
-        def quantise(grouped, codes, scales):
+        def quantise(grouped, codes, scales, c, columns):
             nc.vector.quantize_mx(
-                out=codes.bitcast(FP8X4), scales=scales, in_=grouped[:].rearrange("p c t -> p (c t)")
+                out=codes[:, c, columns].bitcast(FP8X4),
+                scales=scales[:, c, columns],
+                in_=grouped[:].rearrange("p c t -> p (c t)"),
             )
 
-        for b in range(SEQS):
-            for c in range(H_PASSES):
-                h_planes = stage.tile([P, PACK, POS], BF16, name="h_planes")
-                for t in range(PACK):
-                    j = PACK * c + t
-                    units = slice(j * P, (j + 1) * P)
-                    pre = psum.tile([P, POS], F32, tag="bank", name="pre")
-                    for g in range(3):
-                        first = (1 + SHIFT_OF_GROUP[g]) * P
-                        nc.tensor.matmul_mx(
-                            out=pre[:],
-                            lhsT=w_codes[:, g, units].bitcast(FP8X4),
-                            lhsT_scale=w_scales[4 * g : P, units],
-                            rhs=x_codes[:, b, first : first + POS].bitcast(FP8X4),
-                            rhs_scale=x_scales[:, b, first : first + POS],
-                            start=(g == 0),
-                            stop=(g == 2),
-                        )
-                    nc.scalar.activation(out=h_planes[:, t, :], in_=pre[:], func=RELU, bias=bias_cols[:, j : j + 1], scale=1.0)
+        def hidden_planes(b, c):
+            h_planes = stage.tile([P, PACK, POS], BF16, name="h_planes")
+            for t in range(PACK):
+                j = PACK * c + t
+                units = slice(j * P, (j + 1) * P)
+                pre = psum.tile([P, POS], F32, tag="bank", name="pre")
+                for g in range(3):
+                    first = (1 + SHIFT_OF_GROUP[g]) * P
+                    nc.tensor.matmul_mx(
+                        out=pre[:],
+                        lhsT=w_codes[:, g, units].bitcast(FP8X4),
+                        lhsT_scale=w_scales[4 * g : P, units],
+                        rhs=x_codes[:, b, first : first + POS].bitcast(FP8X4),
+                        rhs_scale=x_scales[:, b, first : first + POS],
+                        start=(g == 0),
+                        stop=(g == 2),
+                    )
+                nc.scalar.activation(
+                    out=h_planes[:, t, :], in_=pre[:], func=RELU, bias=bias_cols[:, j : j + 1], scale=1.0
+                )
+            return h_planes
 
-                quarter = H_PASSES * b + c
-                v_map, v_pass = quarter // H_PASSES, quarter % H_PASSES
-                left = slice(v_map * HID, v_map * HID + BANK)
-                right = slice(v_map * HID + BANK, (v_map + 1) * HID)
-                v_left = regroup(nc.vector.tensor_copy, v_raw[quarter][:, :, 0:BANK], "v_left")
-                v_right = regroup(nc.scalar.copy, v_raw[quarter][:, :, BANK:HID], "v_right")
-                h_grouped = regroup(nc.vector.tensor_copy, h_planes[:], "h_grouped")
-                quantise(v_left, v_codes[:, v_pass, left], v_scales[:, v_pass, left])
-                tokens = slice(b * POS, (b + 1) * POS)
-                quantise(h_grouped, h_codes[:, c, tokens], h_scales[:, c, tokens])
-                quantise(v_right, v_codes[:, v_pass, right], v_scales[:, v_pass, right])
+        def map_columns(m, half):
+            return slice(m * HID + half * BANK, m * HID + (half + 1) * BANK)
+
+        for c in range(H_PASSES):
+            h_planes = hidden_planes(0, c)
+            v_left = regroup(v_raw[c][:, :, 0:BANK], "v_grouped")
+            v_right = regroup(v_raw[c][:, :, BANK:HID], "v_grouped")
+            quantise(v_left, v_codes, v_scales, c, map_columns(0, 0))
+            h_grouped = regroup(h_planes[:], "h_grouped")
+            quantise(v_right, v_codes, v_scales, c, map_columns(0, 1))
+            quantise(h_grouped, h_codes, h_scales, c, slice(0, POS))
+
+        h_waiting = []
+        for c in range(H_PASSES):
+            h_planes = hidden_planes(1, c)
+            h_waiting.append(regroup(h_planes[:], "h_grouped"))
+        for c in range(H_PASSES):
+            quantise(h_waiting[c], h_codes, h_scales, c, slice(POS, TOKENS))
+
+        for half in range(HID // BANK):
+            v_waiting = []
+            for c in range(H_PASSES):
+                v_waiting.append(regroup(v_raw[H_PASSES + c][:, :, half * BANK : (half + 1) * BANK], "v_grouped"))
+            for c in range(H_PASSES):
+                quantise(v_waiting[c], v_codes, v_scales, c, map_columns(1, half))
 
         for m in range(MAPS):
             for b in range(SEQS):
@@ -175,20 +198,19 @@ def tile_bilinearpairedlayer_pa_kernel(tc, x_l, W_l_words, W_l_scales, b_l, W_bi
                     tokens = slice(b * POS + r * P, b * POS + (r + 1) * P)
                     result = out_pool.tile([P, HID], F32, name="result")
                     for half in range(HID // BANK):
-                        columns = slice(m * HID + half * BANK, m * HID + (half + 1) * BANK)
                         acc = psum.tile([P, BANK], F32, tag="bank", name="acc")
                         for c in range(H_PASSES):
                             nc.tensor.matmul_mx(
                                 out=acc[:],
                                 lhsT=h_codes[:, c, tokens].bitcast(FP8X4),
                                 lhsT_scale=h_scales[:, c, tokens],
-                                rhs=v_codes[:, c, columns].bitcast(FP8X4),
-                                rhs_scale=v_scales[:, c, columns],
+                                rhs=v_codes[:, c, map_columns(m, half)].bitcast(FP8X4),
+                                rhs_scale=v_scales[:, c, map_columns(m, half)],
                                 start=(c == 0),
                                 stop=(c == H_PASSES - 1),
                             )
-                        if half == 0:
-                            nc.scalar.copy(out=result[:, 0:BANK], in_=acc[:])
+                        if m == 0 or half == 0:
+                            nc.scalar.copy(out=result[:, half * BANK : (half + 1) * BANK], in_=acc[:])
                         else:
-                            nc.vector.tensor_copy(out=result[:, BANK:HID], in_=acc[:])
+                            nc.vector.tensor_copy(out=result[:, half * BANK : (half + 1) * BANK], in_=acc[:])
                     nc.sync.dma_start(out=by_lane[:, r, m, :], in_=result[:])

@@ -191,26 +191,35 @@ def tile_bilinearpairedlayer_pa_kernel(tc, x_l, W_l_words, W_l_scales, b_l, W_bi
             for c in range(H_PASSES):
                 quantise(v_waiting[c], v_codes, v_scales, c, map_columns(1, half))
 
-        for m in range(MAPS):
+        def second_layer_bank(m, half, b, r, copy, target):
+            tokens = slice(b * POS + r * P, b * POS + (r + 1) * P)
+            acc = psum.tile([P, BANK], F32, tag="bank", name="acc")
+            for c in range(H_PASSES):
+                nc.tensor.matmul_mx(
+                    out=acc[:],
+                    lhsT=h_codes[:, c, tokens].bitcast(FP8X4),
+                    lhsT_scale=h_scales[:, c, tokens],
+                    rhs=v_codes[:, c, map_columns(m, half)].bitcast(FP8X4),
+                    rhs_scale=v_scales[:, c, map_columns(m, half)],
+                    start=(c == 0),
+                    stop=(c == H_PASSES - 1),
+                )
+            copy(out=target, in_=acc[:])
+
+        by_lane = out.rearrange("b (a r) m g -> b r m a g", r=LANES)
+
+        for b in range(SEQS):
+            for r in range(LANES):
+                result = out_pool.tile([P, HID], F32, name="result")
+                for half in range(HID // BANK):
+                    second_layer_bank(0, half, b, r, nc.scalar.copy, result[:, half * BANK : (half + 1) * BANK])
+                nc.sync.dma_start(out=by_lane[b, r, 0], in_=result[:])
+
+        for half in range(HID // BANK):
             for b in range(SEQS):
-                by_lane = out[b].rearrange("(a r) m g -> a r m g", r=LANES)
                 for r in range(LANES):
-                    tokens = slice(b * POS + r * P, b * POS + (r + 1) * P)
-                    result = out_pool.tile([P, HID], F32, name="result")
-                    for half in range(HID // BANK):
-                        acc = psum.tile([P, BANK], F32, tag="bank", name="acc")
-                        for c in range(H_PASSES):
-                            nc.tensor.matmul_mx(
-                                out=acc[:],
-                                lhsT=h_codes[:, c, tokens].bitcast(FP8X4),
-                                lhsT_scale=h_scales[:, c, tokens],
-                                rhs=v_codes[:, c, map_columns(m, half)].bitcast(FP8X4),
-                                rhs_scale=v_scales[:, c, map_columns(m, half)],
-                                start=(c == 0),
-                                stop=(c == H_PASSES - 1),
-                            )
-                        if m == 0 or half == 0:
-                            nc.scalar.copy(out=result[:, half * BANK : (half + 1) * BANK], in_=acc[:])
-                        else:
-                            nc.vector.tensor_copy(out=result[:, half * BANK : (half + 1) * BANK], in_=acc[:])
-                    nc.sync.dma_start(out=by_lane[:, r, m, :], in_=result[:])
+                    vector_free = half == 1 or b == 1
+                    copy = nc.vector.tensor_copy if (vector_free and r % 2 == 1) else nc.scalar.copy
+                    result = out_pool.tile([P, BANK], F32, name="half_result")
+                    second_layer_bank(1, half, b, r, copy, result[:])
+                    nc.sync.dma_start(out=by_lane[b, r, 1][:, half * BANK : (half + 1) * BANK], in_=result[:])

@@ -10,7 +10,6 @@ U32 = mybir.dt.uint32
 U8 = mybir.dt.uint8
 FP8X4 = mybir.dt.float8_e4m3fn_x4
 RELU = mybir.ActivationFunctionType.Relu
-IDENTITY = mybir.ActivationFunctionType.Identity
 
 P = 128
 PACK = 4
@@ -44,14 +43,15 @@ def tile_bilinearpairedlayer_pa_kernel(tc, x_l, W_l_words, W_l_scales, b_l, W_bi
         psum = ctx.enter_context(tc.psum_pool(name="psum", bufs=8))
 
         ident = keep.tile([P, P], F32)
+        ident_bf16 = keep.tile([P, P], BF16)
         x_rows = keep.tile([P, SEQS, LANES * FEAT], BF16)
         x_grouped = keep.tile([P, SEQS, SLOTS * P, PACK], BF16, align_bytes=64)
         x_codes = keep.tile([P, SEQS, SLOTS * P], U32, align_bytes=64)
         x_scales = keep.tile([P, SEQS, SLOTS * P], U8, align_bytes=64)
         w_codes = keep.tile([P, 3, HID], U32, align_bytes=64)
-        w_scales = keep.tile([P, HID], U8, align_bytes=64)
+        w_scales = keep.tile([P, 3, HID], U8, align_bytes=64)
+        table_probe = keep.tile([P, 2], F32)
         bias_rows = keep.tile([P, P], BF16)
-        bias_rows_f32 = keep.tile([P, P], F32)
         bias_cols = keep.tile([P, H_TILES], F32)
         h_codes = keep.tile([P, H_PASSES, TOKENS], U32, align_bytes=64)
         h_scales = keep.tile([P, H_PASSES, TOKENS], U8, align_bytes=64)
@@ -61,71 +61,97 @@ def tile_bilinearpairedlayer_pa_kernel(tc, x_l, W_l_words, W_l_scales, b_l, W_bi
         x_words = x_rows[:].bitcast(F32)
         x_grouped_words = x_grouped[:].bitcast(F32)
 
-        nc.vector.memset(w_scales[:].bitcast(I32), 0)
         nc.vector.memset(bias_rows[:], 0.0)
+        nc.vector.memset(table_probe[:], 0.0)
+        nc.vector.memset(w_scales[:].bitcast(I32), 0)
         nc.vector.memset(x_grouped_words[:, :, 0:4, :], 0.0)
         nc.vector.memset(x_grouped_words[:, :, SLOTS * P - 4 : SLOTS * P, :], 0.0)
         make_identity(nc, ident[:])
+        make_identity(nc, ident_bf16[:])
 
-        nc.scalar.dma_start(out=bias_rows[0:H_TILES, :], in_=b_l.rearrange("(j p) -> j p", p=P))
-        nc.sync.dma_start(out=x_rows[:, 0, :], in_=x_l[0].rearrange("(a r) k -> a (r k)", r=LANES))
+        x_by_lane = x_l.rearrange("b (a r) k -> b a (r k)", r=LANES)
+        for pair in range(LANES // 2):
+            columns = slice(pair * 2 * FEAT, (pair + 1) * 2 * FEAT)
+            nc.sync.dma_start(out=x_rows[:, 0, columns], in_=x_by_lane[0][:, columns])
+            if pair == 0:
+                nc.sync.dma_start(out=bias_rows[0:H_TILES, :], in_=b_l.rearrange("(j p) -> j p", p=P))
+        nc.sync.dma_start(out=x_rows[:, 1, :], in_=x_by_lane[1])
+        w_bytes = W_l_words.rearrange("g p n t -> p g (n t)")
+
+        def load_w(c):
+            nc.sync.dma_start(
+                out=w_codes[:, :, c * K_PASS : (c + 1) * K_PASS].bitcast(I32),
+                in_=w_bytes[:, :, c * K_PASS * PACK : (c + 1) * K_PASS * PACK].bitcast(I32),
+            )
+
+        def load_v(m, c):
+            raw = raw_pool.tile([P, PACK, HID], BF16, name="raw")
+            nc.sync.dma_start(out=raw[:], in_=W_bil[m].rearrange("(c t p) n -> c p t n", t=PACK, p=P)[c])
+            return raw
+
+        load_w(0)
         for quad in range(4):
             nc.sync.dma_start(
-                out=w_scales[32 * quad : 32 * quad + 12, :].bitcast(I32),
-                in_=W_l_scales[:, 4 * quad : 4 * quad + 4, :].bitcast(I32),
+                out=w_scales[32 * quad : 32 * quad + 4, :, :].bitcast(I32),
+                in_=W_l_scales[:, 4 * quad : 4 * quad + 4, :].rearrange("g q n -> q g n").bitcast(I32),
             )
-        nc.sync.dma_start(out=x_rows[:, 1, :], in_=x_l[1].rearrange("(a r) k -> a (r k)", r=LANES))
-        w_bytes = W_l_words.rearrange("g p n t -> p g (n t)")
-        v_raw = []
-        for m in range(MAPS):
-            by_pass = W_bil[m].rearrange("(c t p) n -> c p t n", t=PACK, p=P)
-            for c in range(H_PASSES):
-                if m == 0:
-                    nc.sync.dma_start(
-                        out=w_codes[:, :, c * K_PASS : (c + 1) * K_PASS].bitcast(I32),
-                        in_=w_bytes[:, :, c * K_PASS * PACK : (c + 1) * K_PASS * PACK].bitcast(I32),
-                    )
-                raw = raw_pool.tile([P, PACK, HID], BF16, name="raw")
-                nc.sync.dma_start(out=raw[:], in_=by_pass[c])
-                v_raw.append(raw)
+        v_raw = [load_v(0, 0)]
+        load_w(1)
+        v_raw.append(load_v(0, 1))
+        v_raw.append(load_v(1, 0))
+        v_raw.append(load_v(1, 1))
 
-        nc.scalar.activation(out=bias_rows_f32[:], in_=bias_rows[:], func=IDENTITY)
+        nc.scalar.activation(out=table_probe[:, 1:2], in_=table_probe[:, 0:1], func=RELU)
 
-        for b in range(SEQS):
-            for pair in range(LANES // 2):
-                flipped = psum.tile([P, 2, 2, P], F32, tag="bank", name="flipped")
-                for s in range(2):
-                    first = (2 * pair + s) * (FEAT // 2)
-                    for u in range(2):
-                        nc.tensor.transpose(
-                            out=flipped[:, s, u, :],
-                            in_=x_words[:, b, first + u : first + FEAT // 2 : 2],
-                            identity=ident[:],
-                        )
-                columns = slice((1 + 2 * pair) * P, (3 + 2 * pair) * P)
-                target = x_grouped_words[:, b, columns, :].rearrange("p (s a) u -> p s a u", s=2)
-                source = flipped[:].rearrange("p s u a -> p s a u")
-                if pair == 0:
-                    nc.vector.tensor_copy(out=target, in_=source)
-                    nc.vector.tensor_copy(
-                        out=x_grouped_words[:, b, (LANES + 1) * P : SLOTS * P - 1, :],
-                        in_=flipped[:, 0, :, 1:P].rearrange("p u a -> p a u"),
+        def flip(b, pair):
+            flipped = psum.tile([P, 2, 2, P], F32, tag="bank", name="flipped")
+            for s in range(2):
+                first = (2 * pair + s) * (FEAT // 2)
+                for u in range(2):
+                    nc.tensor.transpose(
+                        out=flipped[:, s, u, :],
+                        in_=x_words[:, b, first + u : first + FEAT // 2 : 2],
+                        identity=ident[:],
                     )
-                else:
-                    nc.scalar.copy(out=target, in_=source)
-                    nc.scalar.copy(
-                        out=x_grouped_words[:, b, 1:P, :],
-                        in_=flipped[:, 1, :, 0 : P - 1].rearrange("p u a -> p a u"),
-                    )
-            for columns in (slice(0, LANES * P), slice(LANES * P, SLOTS * P)):
-                nc.vector.quantize_mx(
-                    out=x_codes[:, b, columns].bitcast(FP8X4),
-                    scales=x_scales[:, b, columns],
-                    in_=x_grouped[:, b, columns, :].rearrange("p c t -> p (c t)"),
+            return flipped
+
+        def place(b, pair, flipped):
+            columns = slice((1 + 2 * pair) * P, (3 + 2 * pair) * P)
+            target = x_grouped_words[:, b, columns, :].rearrange("p (s a) u -> p s a u", s=2)
+            source = flipped[:].rearrange("p s u a -> p s a u")
+            if pair == 0:
+                nc.vector.tensor_copy(out=target, in_=source)
+                nc.vector.tensor_copy(
+                    out=x_grouped_words[:, b, (LANES + 1) * P : SLOTS * P - 1, :],
+                    in_=flipped[:, 0, :, 1:P].rearrange("p u a -> p a u"),
+                )
+            else:
+                nc.scalar.copy(out=target, in_=source)
+                nc.scalar.copy(
+                    out=x_grouped_words[:, b, 1:P, :], in_=flipped[:, 1, :, 0 : P - 1].rearrange("p u a -> p a u")
                 )
 
-        bias_flipped = psum.tile([P, P], F32, tag="bank", name="bias_flipped")
-        nc.tensor.transpose(out=bias_flipped[:], in_=bias_rows_f32[:], identity=ident[:])
+        def quantise_x(b, columns):
+            nc.vector.quantize_mx(
+                out=x_codes[:, b, columns].bitcast(FP8X4),
+                scales=x_scales[:, b, columns],
+                in_=x_grouped[:, b, columns, :].rearrange("p c t -> p (c t)"),
+            )
+
+        def prepare_x(b):
+            for pair in range(LANES // 2):
+                flipped = flip(b, pair)
+                place(b, pair, flipped)
+            quantise_x(b, slice(P, 3 * P))
+            quantise_x(b, slice(3 * P, 5 * P))
+            quantise_x(b, slice(0, P))
+            quantise_x(b, slice(5 * P, 6 * P))
+
+        prepare_x(0)
+        prepare_x(1)
+
+        bias_flipped = psum.tile([P, P], BF16, tag="bank", name="bias_flipped")
+        nc.tensor.transpose(out=bias_flipped[:], in_=bias_rows[:], identity=ident_bf16[:])
         nc.scalar.copy(out=bias_cols[:], in_=bias_flipped[:, 0:H_TILES])
 
         def regroup(planes, name):
@@ -143,53 +169,30 @@ def tile_bilinearpairedlayer_pa_kernel(tc, x_l, W_l_words, W_l_scales, b_l, W_bi
                 in_=grouped[:].rearrange("p c t -> p (c t)"),
             )
 
-        def hidden_planes(b, c):
-            h_planes = stage.tile([P, PACK, POS], BF16, name="h_planes")
-            for t in range(PACK):
-                j = PACK * c + t
-                units = slice(j * P, (j + 1) * P)
-                pre = psum.tile([P, POS], F32, tag="bank", name="pre")
-                for g in range(3):
-                    first = (1 + SHIFT_OF_GROUP[g]) * P
-                    nc.tensor.matmul_mx(
-                        out=pre[:],
-                        lhsT=w_codes[:, g, units].bitcast(FP8X4),
-                        lhsT_scale=w_scales[4 * g : P, units],
-                        rhs=x_codes[:, b, first : first + POS].bitcast(FP8X4),
-                        rhs_scale=x_scales[:, b, first : first + POS],
-                        start=(g == 0),
-                        stop=(g == 2),
-                    )
-                nc.scalar.activation(
-                    out=h_planes[:, t, :], in_=pre[:], func=RELU, bias=bias_cols[:, j : j + 1], scale=1.0
+        def hidden_tile(b, c, t, h_planes):
+            j = PACK * c + t
+            units = slice(j * P, (j + 1) * P)
+            pre = psum.tile([P, POS], F32, tag="bank", name="pre")
+            for g in range(3):
+                first = (1 + SHIFT_OF_GROUP[g]) * P
+                nc.tensor.matmul_mx(
+                    out=pre[:],
+                    lhsT=w_codes[:, g, units].bitcast(FP8X4),
+                    lhsT_scale=w_scales[:, g, units],
+                    rhs=x_codes[:, b, first : first + POS].bitcast(FP8X4),
+                    rhs_scale=x_scales[:, b, first : first + POS],
+                    start=(g == 0),
+                    stop=(g == 2),
                 )
-            return h_planes
+            nc.scalar.activation(
+                out=h_planes[:, t, :], in_=pre[:], func=RELU, bias=bias_cols[:, j : j + 1], scale=1.0
+            )
 
         def map_columns(m, half):
             return slice(m * HID + half * BANK, m * HID + (half + 1) * BANK)
 
-        for c in range(H_PASSES):
-            h_planes = hidden_planes(0, c)
-            v_left = regroup(v_raw[c][:, :, 0:BANK], "v_grouped")
-            v_right = regroup(v_raw[c][:, :, BANK:HID], "v_grouped")
-            quantise(v_left, v_codes, v_scales, c, map_columns(0, 0))
-            h_grouped = regroup(h_planes[:], "h_grouped")
-            quantise(v_right, v_codes, v_scales, c, map_columns(0, 1))
-            quantise(h_grouped, h_codes, h_scales, c, slice(0, POS))
-
-        h_waiting = []
-        for c in range(H_PASSES):
-            h_planes = hidden_planes(1, c)
-            h_waiting.append(regroup(h_planes[:], "h_grouped"))
-        for c in range(H_PASSES):
-            quantise(h_waiting[c], h_codes, h_scales, c, slice(POS, TOKENS))
-
-        for half in range(HID // BANK):
-            v_waiting = []
-            for c in range(H_PASSES):
-                v_waiting.append(regroup(v_raw[H_PASSES + c][:, :, half * BANK : (half + 1) * BANK], "v_grouped"))
-            for c in range(H_PASSES):
-                quantise(v_waiting[c], v_codes, v_scales, c, map_columns(1, half))
+        def v_half(m, c, half):
+            return v_raw[H_PASSES * m + c][:, :, half * BANK : (half + 1) * BANK]
 
         def second_layer_bank(m, half, b, r, copy, target):
             tokens = slice(b * POS + r * P, b * POS + (r + 1) * P)
@@ -208,18 +211,69 @@ def tile_bilinearpairedlayer_pa_kernel(tc, x_l, W_l_words, W_l_scales, b_l, W_bi
 
         by_lane = out.rearrange("b (a r) m g -> b r m a g", r=LANES)
 
-        for b in range(SEQS):
-            for r in range(LANES):
-                result = out_pool.tile([P, HID], F32, name="result")
-                for half in range(HID // BANK):
-                    second_layer_bank(0, half, b, r, nc.scalar.copy, result[:, half * BANK : (half + 1) * BANK])
-                nc.sync.dma_start(out=by_lane[b, r, 0], in_=result[:])
+        def store_half(m, half, b, r, copy):
+            result = out_pool.tile([P, BANK], F32, name="half_result")
+            second_layer_bank(m, half, b, r, copy, result[:])
+            nc.sync.dma_start(out=by_lane[b, r, m][:, half * BANK : (half + 1) * BANK], in_=result[:])
 
-        for half in range(HID // BANK):
-            for b in range(SEQS):
-                for r in range(LANES):
-                    vector_free = half == 1 or b == 1
-                    copy = nc.vector.tensor_copy if (vector_free and r % 2 == 1) else nc.scalar.copy
-                    result = out_pool.tile([P, BANK], F32, name="half_result")
-                    second_layer_bank(1, half, b, r, copy, result[:])
-                    nc.sync.dma_start(out=by_lane[b, r, 1][:, half * BANK : (half + 1) * BANK], in_=result[:])
+        def store_lane(m, b, r, copies):
+            result = out_pool.tile([P, HID], F32, name="result")
+            for half in range(HID // BANK):
+                second_layer_bank(m, half, b, r, copies[half], result[:, half * BANK : (half + 1) * BANK])
+            nc.sync.dma_start(out=by_lane[b, r, m], in_=result[:])
+
+        on_scalar = nc.scalar.copy
+        on_vector = nc.vector.tensor_copy
+
+        def hidden_planes(b, c):
+            h_planes = stage.tile([P, PACK, POS], BF16, name="h_planes")
+            for t in range(PACK):
+                hidden_tile(b, c, t, h_planes)
+            return h_planes
+
+        def quantise_v(grouped, m, c, half):
+            quantise(grouped, v_codes, v_scales, c, map_columns(m, half))
+
+        def quantise_h(grouped, b, c):
+            quantise(grouped, h_codes, h_scales, c, slice(b * POS, (b + 1) * POS))
+
+        h_00 = hidden_planes(0, 0)
+        v_000 = regroup(v_half(0, 0, 0), "v_grouped")
+        v_001 = regroup(v_half(0, 0, 1), "v_grouped")
+        quantise_v(v_000, 0, 0, 0)
+        hg_00 = regroup(h_00[:], "h_grouped")
+        quantise_v(v_001, 0, 0, 1)
+        h_01 = hidden_planes(0, 1)
+        v_010 = regroup(v_half(0, 1, 0), "v_grouped")
+        quantise_h(hg_00, 0, 0)
+        hg_01 = regroup(h_01[:], "h_grouped")
+        quantise_v(v_010, 0, 1, 0)
+        v_011 = regroup(v_half(0, 1, 1), "v_grouped")
+        quantise_h(hg_01, 0, 1)
+        h_10 = hidden_planes(1, 0)
+        hg_10 = regroup(h_10[:], "h_grouped")
+        quantise_v(v_011, 0, 1, 1)
+        v_100 = regroup(v_half(1, 0, 0), "v_grouped")
+        quantise_h(hg_10, 1, 0)
+        h_11 = hidden_planes(1, 1)
+        v_110 = regroup(v_half(1, 1, 0), "v_grouped")
+        quantise_v(v_100, 1, 0, 0)
+        hg_11 = regroup(h_11[:], "h_grouped")
+        quantise_v(v_110, 1, 1, 0)
+        v_101 = regroup(v_half(1, 0, 1), "v_grouped")
+        quantise_h(hg_11, 1, 1)
+        v_111 = regroup(v_half(1, 1, 1), "v_grouped")
+        quantise_v(v_101, 1, 0, 1)
+        quantise_v(v_111, 1, 1, 1)
+
+        for r in range(LANES):
+            store_lane(0, 0, r, (on_scalar, on_scalar))
+        for r in range(LANES):
+            store_half(1, 0, 0, r, on_scalar)
+        for r in range(LANES):
+            store_lane(0, 1, r, (on_scalar, on_vector if r >= 2 else on_scalar))
+        for r in range(LANES):
+            store_half(1, 1, 0, r, on_vector if r % 2 == 0 else on_scalar)
+        for r in range(LANES):
+            for half in range(HID // BANK):
+                store_half(1, half, 1, r, on_vector if half == 0 else on_scalar)

@@ -45,12 +45,14 @@ def tile_bilinearpairedlayer_pa_kernel(tc, x_l, W_l_words, W_l_scales, b_l, W_bi
         ident = keep.tile([P, P], F32)
         ident_bf16 = keep.tile([P, P], BF16)
         x_rows = keep.tile([P, SEQS, LANES * FEAT], BF16)
+        x_halves = keep.tile([P, SEQS, LANES * FEAT // 2], F32)
         x_grouped = keep.tile([P, SEQS, SLOTS * P, PACK], BF16, align_bytes=64)
         x_codes = keep.tile([P, SEQS, SLOTS * P], U32, align_bytes=64)
         x_scales = keep.tile([P, SEQS, SLOTS * P], U8, align_bytes=64)
         w_codes = keep.tile([P, 3, HID], U32, align_bytes=64)
         w_scales = keep.tile([P, 3, HID], U8, align_bytes=64)
         table_probe = keep.tile([P, 2], F32)
+        blank = keep.tile([P, BANK], BF16)
         bias_rows = keep.tile([P, P], BF16)
         bias_cols = keep.tile([P, H_TILES], F32)
         h_codes = keep.tile([P, H_PASSES, TOKENS], U32, align_bytes=64)
@@ -61,6 +63,7 @@ def tile_bilinearpairedlayer_pa_kernel(tc, x_l, W_l_words, W_l_scales, b_l, W_bi
         x_words = x_rows[:].bitcast(F32)
         x_grouped_words = x_grouped[:].bitcast(F32)
 
+        nc.gpsimd.memset(blank[:], 0.0)
         nc.vector.memset(bias_rows[:], 0.0)
         nc.vector.memset(table_probe[:], 0.0)
         nc.vector.memset(w_scales[:].bitcast(I32), 0)
@@ -73,8 +76,7 @@ def tile_bilinearpairedlayer_pa_kernel(tc, x_l, W_l_words, W_l_scales, b_l, W_bi
         for pair in range(LANES // 2):
             columns = slice(pair * 2 * FEAT, (pair + 1) * 2 * FEAT)
             nc.sync.dma_start(out=x_rows[:, 0, columns], in_=x_by_lane[0][:, columns])
-            if pair == 0:
-                nc.sync.dma_start(out=bias_rows[0:H_TILES, :], in_=b_l.rearrange("(j p) -> j p", p=P))
+        nc.sync.dma_start(out=bias_rows[0:H_TILES, :], in_=b_l.rearrange("(j p) -> j p", p=P))
         nc.sync.dma_start(out=x_rows[:, 1, :], in_=x_by_lane[1])
         w_bytes = W_l_words.rearrange("g p n t -> p g (n t)")
 
@@ -103,14 +105,26 @@ def tile_bilinearpairedlayer_pa_kernel(tc, x_l, W_l_words, W_l_scales, b_l, W_bi
 
         nc.scalar.activation(out=table_probe[:, 1:2], in_=table_probe[:, 0:1], func=RELU)
 
+        def keep_busy(count):
+            for step in range(count):
+                idle = psum.tile([P, BANK], F32, tag="bank", name="idle")
+                nc.tensor.matmul(out=idle[:], lhsT=blank[:, 0:P], rhs=blank[:], start=True, stop=True)
+
+        def split_words(b, pairs):
+            words = slice(pairs.start * FEAT, pairs.stop * FEAT)
+            nc.vector.tensor_copy(
+                out=x_halves[:, b, words].rearrange("a (r u p) -> a r u p", u=2, p=P),
+                in_=x_words[:, b, words].rearrange("a (r p u) -> a r u p", u=2, p=P),
+            )
+
         def flip(b, pair):
             flipped = psum.tile([P, 2, 2, P], F32, tag="bank", name="flipped")
             for s in range(2):
-                first = (2 * pair + s) * (FEAT // 2)
+                first = (2 * pair + s) * 2 * P
                 for u in range(2):
                     nc.tensor.transpose(
                         out=flipped[:, s, u, :],
-                        in_=x_words[:, b, first + u : first + FEAT // 2 : 2],
+                        in_=x_halves[:, b, first + u * P : first + (u + 1) * P],
                         identity=ident[:],
                     )
             return flipped
@@ -138,21 +152,33 @@ def tile_bilinearpairedlayer_pa_kernel(tc, x_l, W_l_words, W_l_scales, b_l, W_bi
                 in_=x_grouped[:, b, columns, :].rearrange("p c t -> p (c t)"),
             )
 
-        def prepare_x(b):
-            for pair in range(LANES // 2):
-                flipped = flip(b, pair)
-                place(b, pair, flipped)
-            quantise_x(b, slice(P, 3 * P))
+        def quantise_rest_of_x(b):
             quantise_x(b, slice(3 * P, 5 * P))
             quantise_x(b, slice(0, P))
             quantise_x(b, slice(5 * P, 6 * P))
 
-        prepare_x(0)
-        prepare_x(1)
+        keep_busy(6)
+        split_words(0, slice(0, 1))
+        split_words(0, slice(1, 2))
+        flipped_00 = flip(0, 0)
+        flipped_01 = flip(0, 1)
+        keep_busy(2)
+        place(0, 0, flipped_00)
+        place(0, 1, flipped_01)
+        quantise_x(0, slice(P, 3 * P))
+        split_words(1, slice(0, 2))
+        flipped_10 = flip(1, 0)
+        flipped_11 = flip(1, 1)
+        quantise_rest_of_x(0)
 
         bias_flipped = psum.tile([P, P], BF16, tag="bank", name="bias_flipped")
         nc.tensor.transpose(out=bias_flipped[:], in_=bias_rows[:], identity=ident_bf16[:])
         nc.scalar.copy(out=bias_cols[:], in_=bias_flipped[:, 0:H_TILES])
+        keep_busy(1)
+        place(1, 0, flipped_10)
+        place(1, 1, flipped_11)
+        quantise_x(1, slice(P, 3 * P))
+        quantise_rest_of_x(1)
 
         def regroup(planes, name):
             grouped = stage.tile([P, BANK, PACK], BF16, align_bytes=64, name=name)

@@ -220,16 +220,17 @@ def tile_bilinearpairedlayer_pa_kernel(tc, x_l, W_l_words, W_l_scales, b_l, W_bi
         def v_half(m, c, half):
             return v_raw[H_PASSES * m + c][:, :, half * BANK : (half + 1) * BANK]
 
-        def second_layer_bank(m, half, b, r, copy, target):
+        def second_layer(m, columns, b, r, copy, target):
             tokens = slice(b * POS + r * P, b * POS + (r + 1) * P)
-            acc = psum.tile([P, BANK], F32, tag="bank", name="acc")
+            of_maps = slice(m * HID + columns.start, m * HID + columns.stop)
+            acc = psum.tile([P, columns.stop - columns.start], F32, tag="bank", name="acc")
             for c in range(H_PASSES):
                 nc.tensor.matmul_mx(
                     out=acc[:],
                     lhsT=h_codes[:, c, tokens].bitcast(FP8X4),
                     lhsT_scale=h_scales[:, c, tokens],
-                    rhs=v_codes[:, c, map_columns(m, half)].bitcast(FP8X4),
-                    rhs_scale=v_scales[:, c, map_columns(m, half)],
+                    rhs=v_codes[:, c, of_maps].bitcast(FP8X4),
+                    rhs_scale=v_scales[:, c, of_maps],
                     start=(c == 0),
                     stop=(c == H_PASSES - 1),
                 )
@@ -237,15 +238,20 @@ def tile_bilinearpairedlayer_pa_kernel(tc, x_l, W_l_words, W_l_scales, b_l, W_bi
 
         by_lane = out.rearrange("b (a r) m g -> b r m a g", r=LANES)
 
+        def store_part(m, first, width, b, r, copy):
+            result = out_pool.tile([P, width], F32, name="part_%d" % width)
+            columns = slice(first, first + width)
+            second_layer(m, columns, b, r, copy, result[:])
+            nc.sync.dma_start(out=by_lane[b, r, m][:, columns], in_=result[:])
+
         def store_half(m, half, b, r, copy):
-            result = out_pool.tile([P, BANK], F32, name="half_result")
-            second_layer_bank(m, half, b, r, copy, result[:])
-            nc.sync.dma_start(out=by_lane[b, r, m][:, half * BANK : (half + 1) * BANK], in_=result[:])
+            store_part(m, half * BANK, BANK, b, r, copy)
 
         def store_lane(m, b, r, copies):
             result = out_pool.tile([P, HID], F32, name="result")
             for half in range(HID // BANK):
-                second_layer_bank(m, half, b, r, copies[half], result[:, half * BANK : (half + 1) * BANK])
+                columns = slice(half * BANK, (half + 1) * BANK)
+                second_layer(m, columns, b, r, copies[half], result[:, columns])
             nc.sync.dma_start(out=by_lane[b, r, m], in_=result[:])
 
         on_scalar = nc.scalar.copy
@@ -281,11 +287,19 @@ def tile_bilinearpairedlayer_pa_kernel(tc, x_l, W_l_words, W_l_scales, b_l, W_bi
         quantise_v(v_011, 0, 1, 1)
         v_100 = regroup(v_half(1, 0, 0), "v_grouped")
         quantise_h(hg_10, 1, 0)
-        h_11 = hidden_planes(1, 1)
+        h_11 = stage.tile([P, PACK, POS], BF16, name="h_planes")
+        hidden_tile(1, 1, 0, h_11)
+        hidden_tile(1, 1, 1, h_11)
+        store_lane(0, 0, 0, (on_scalar, on_scalar))
+        hidden_tile(1, 1, 2, h_11)
+        store_lane(0, 0, 1, (on_scalar, on_scalar))
+        hidden_tile(1, 1, 3, h_11)
+        store_lane(0, 0, 2, (on_scalar, on_scalar))
+        store_lane(0, 0, 3, (on_scalar, on_scalar))
         v_110 = regroup(v_half(1, 1, 0), "v_grouped")
         quantise_v(v_100, 1, 0, 0)
-        hg_11 = regroup(h_11[:], "h_grouped")
         quantise_v(v_110, 1, 1, 0)
+        hg_11 = regroup(h_11[:], "h_grouped")
         v_101 = regroup(v_half(1, 0, 1), "v_grouped")
         quantise_h(hg_11, 1, 1)
         v_111 = regroup(v_half(1, 1, 1), "v_grouped")
@@ -293,13 +307,13 @@ def tile_bilinearpairedlayer_pa_kernel(tc, x_l, W_l_words, W_l_scales, b_l, W_bi
         quantise_v(v_111, 1, 1, 1)
 
         for r in range(LANES):
-            store_lane(0, 0, r, (on_scalar, on_scalar))
-        for r in range(LANES):
             store_half(1, 0, 0, r, on_scalar)
         for r in range(LANES):
             store_lane(0, 1, r, (on_scalar, on_vector if r >= 2 else on_scalar))
         for r in range(LANES):
             store_half(1, 1, 0, r, on_vector if r % 2 == 0 else on_scalar)
-        for r in range(LANES):
-            for half in range(HID // BANK):
-                store_half(1, half, 1, r, on_vector if half == 0 else on_scalar)
+        for r in range(LANES - 1):
+            store_lane(1, 1, r, (on_vector, on_scalar))
+        store_half(1, 0, 1, LANES - 1, on_vector)
+        store_part(1, BANK, BANK // 2, 1, LANES - 1, on_scalar)
+        store_part(1, BANK + BANK // 2, BANK // 2, 1, LANES - 1, on_vector)

@@ -37,9 +37,9 @@ def tile_bilinearpairedlayer_pa_kernel(tc, x_l, W_l_words, W_l_scales, b_l, W_bi
     with ExitStack() as ctx:
         ctx.enter_context(tc.manual_schedule())
         keep = ctx.enter_context(tc.tile_pool(name="keep", bufs=1))
-        raw_pool = ctx.enter_context(tc.tile_pool(name="raw", bufs=MAPS * H_PASSES))
+        raw_pool = ctx.enter_context(tc.tile_pool(name="raw", bufs=3))
         stage = ctx.enter_context(tc.tile_pool(name="stage", bufs=3))
-        out_pool = ctx.enter_context(tc.tile_pool(name="outs", bufs=8))
+        out_pool = ctx.enter_context(tc.tile_pool(name="outs", bufs=16))
         psum = ctx.enter_context(tc.psum_pool(name="psum", bufs=8))
 
         ident = keep.tile([P, P], F32)
@@ -63,7 +63,7 @@ def tile_bilinearpairedlayer_pa_kernel(tc, x_l, W_l_words, W_l_scales, b_l, W_bi
         x_words = x_rows[:].bitcast(F32)
         x_grouped_words = x_grouped[:].bitcast(F32)
 
-        nc.gpsimd.memset(blank[:], 0.0)
+        nc.vector.memset(blank[:], 0.0)
         nc.vector.memset(bias_rows[:], 0.0)
         nc.vector.memset(table_probe[:], 0.0)
         nc.vector.memset(w_scales[:].bitcast(I32), 0)
@@ -77,7 +77,6 @@ def tile_bilinearpairedlayer_pa_kernel(tc, x_l, W_l_words, W_l_scales, b_l, W_bi
             columns = slice(pair * 2 * FEAT, (pair + 1) * 2 * FEAT)
             nc.sync.dma_start(out=x_rows[:, 0, columns], in_=x_by_lane[0][:, columns])
         nc.sync.dma_start(out=bias_rows[0:H_TILES, :], in_=b_l.rearrange("(j p) -> j p", p=P))
-        nc.sync.dma_start(out=x_rows[:, 1, :], in_=x_by_lane[1])
         w_bytes = W_l_words.rearrange("g p n t -> p g (n t)")
 
         def load_w(c):
@@ -86,10 +85,16 @@ def tile_bilinearpairedlayer_pa_kernel(tc, x_l, W_l_words, W_l_scales, b_l, W_bi
                 in_=w_bytes[:, :, c * K_PASS * PACK : (c + 1) * K_PASS * PACK].bitcast(I32),
             )
 
-        def load_v(m, c):
-            raw = raw_pool.tile([P, PACK, HID], BF16, name="raw")
-            nc.sync.dma_start(out=raw[:], in_=W_bil[m].rearrange("(c t p) n -> c p t n", t=PACK, p=P)[c])
-            return raw
+        v_raw = {}
+
+        def load_v(m, c, halves):
+            columns = slice(halves[0] * BANK, (halves[-1] + 1) * BANK)
+            raw = raw_pool.tile([P, PACK, len(halves) * BANK], BF16, name="raw_%d" % len(halves))
+            nc.sync.dma_start(
+                out=raw[:], in_=W_bil[m].rearrange("(c t p) n -> c p t n", t=PACK, p=P)[c][:, :, columns]
+            )
+            for i, half in enumerate(halves):
+                v_raw[m, c, half] = raw[:, :, i * BANK : (i + 1) * BANK]
 
         load_w(0)
         for quad in range(4):
@@ -97,11 +102,13 @@ def tile_bilinearpairedlayer_pa_kernel(tc, x_l, W_l_words, W_l_scales, b_l, W_bi
                 out=w_scales[32 * quad : 32 * quad + 4, :, :].bitcast(I32),
                 in_=W_l_scales[:, 4 * quad : 4 * quad + 4, :].rearrange("g q n -> q g n").bitcast(I32),
             )
-        v_raw = [load_v(0, 0)]
+        load_v(0, 0, (0,))
+        nc.sync.dma_start(out=x_rows[:, 1, :], in_=x_by_lane[1])
+        load_v(0, 0, (1,))
         load_w(1)
-        v_raw.append(load_v(0, 1))
-        v_raw.append(load_v(1, 0))
-        v_raw.append(load_v(1, 1))
+        load_v(0, 1, (0, 1))
+        load_v(1, 0, (0, 1))
+        load_v(1, 1, (0, 1))
 
         nc.scalar.activation(out=table_probe[:, 1:2], in_=table_probe[:, 0:1], func=RELU)
 
@@ -129,19 +136,19 @@ def tile_bilinearpairedlayer_pa_kernel(tc, x_l, W_l_words, W_l_scales, b_l, W_bi
                     )
             return flipped
 
-        def place(b, pair, flipped):
+        def place(b, pair, flipped, copy):
             columns = slice((1 + 2 * pair) * P, (3 + 2 * pair) * P)
             target = x_grouped_words[:, b, columns, :].rearrange("p (s a) u -> p s a u", s=2)
             source = flipped[:].rearrange("p s u a -> p s a u")
             if pair == 0:
-                nc.vector.tensor_copy(out=target, in_=source)
-                nc.vector.tensor_copy(
+                copy(out=target, in_=source)
+                copy(
                     out=x_grouped_words[:, b, (LANES + 1) * P : SLOTS * P - 1, :],
                     in_=flipped[:, 0, :, 1:P].rearrange("p u a -> p a u"),
                 )
             else:
-                nc.scalar.copy(out=target, in_=source)
-                nc.scalar.copy(
+                copy(out=target, in_=source)
+                copy(
                     out=x_grouped_words[:, b, 1:P, :], in_=flipped[:, 1, :, 0 : P - 1].rearrange("p u a -> p a u")
                 )
 
@@ -152,33 +159,23 @@ def tile_bilinearpairedlayer_pa_kernel(tc, x_l, W_l_words, W_l_scales, b_l, W_bi
                 in_=x_grouped[:, b, columns, :].rearrange("p c t -> p (c t)"),
             )
 
-        def quantise_rest_of_x(b):
-            quantise_x(b, slice(3 * P, 5 * P))
-            quantise_x(b, slice(0, P))
-            quantise_x(b, slice(5 * P, 6 * P))
-
-        keep_busy(6)
+        keep_busy(4)
         split_words(0, slice(0, 1))
         split_words(0, slice(1, 2))
         flipped_00 = flip(0, 0)
         flipped_01 = flip(0, 1)
-        keep_busy(2)
-        place(0, 0, flipped_00)
-        place(0, 1, flipped_01)
-        quantise_x(0, slice(P, 3 * P))
-        split_words(1, slice(0, 2))
-        flipped_10 = flip(1, 0)
-        flipped_11 = flip(1, 1)
-        quantise_rest_of_x(0)
 
         bias_flipped = psum.tile([P, P], BF16, tag="bank", name="bias_flipped")
         nc.tensor.transpose(out=bias_flipped[:], in_=bias_rows[:], identity=ident_bf16[:])
+        keep_busy(3)
+
+        place(0, 0, flipped_00, nc.vector.tensor_copy)
+        place(0, 1, flipped_01, nc.scalar.copy)
         nc.scalar.copy(out=bias_cols[:], in_=bias_flipped[:, 0:H_TILES])
-        keep_busy(1)
-        place(1, 0, flipped_10)
-        place(1, 1, flipped_11)
-        quantise_x(1, slice(P, 3 * P))
-        quantise_rest_of_x(1)
+        quantise_x(0, slice(P, 3 * P))
+        quantise_x(0, slice(3 * P, 5 * P))
+        quantise_x(0, slice(0, P))
+        quantise_x(0, slice(5 * P, 6 * P))
 
         def regroup(planes, name):
             grouped = stage.tile([P, BANK, PACK], BF16, align_bytes=64, name=name)
@@ -217,9 +214,6 @@ def tile_bilinearpairedlayer_pa_kernel(tc, x_l, W_l_words, W_l_scales, b_l, W_bi
         def map_columns(m, half):
             return slice(m * HID + half * BANK, m * HID + (half + 1) * BANK)
 
-        def v_half(m, c, half):
-            return v_raw[H_PASSES * m + c][:, :, half * BANK : (half + 1) * BANK]
-
         def second_layer(m, columns, b, r, copy, target):
             tokens = slice(b * POS + r * P, b * POS + (r + 1) * P)
             of_maps = slice(m * HID + columns.start, m * HID + columns.stop)
@@ -247,13 +241,6 @@ def tile_bilinearpairedlayer_pa_kernel(tc, x_l, W_l_words, W_l_scales, b_l, W_bi
         def store_half(m, half, b, r, copy):
             store_part(m, half * BANK, BANK, b, r, copy)
 
-        def store_lane(m, b, r, copies):
-            result = out_pool.tile([P, HID], F32, name="result")
-            for half in range(HID // BANK):
-                columns = slice(half * BANK, (half + 1) * BANK)
-                second_layer(m, columns, b, r, copies[half], result[:, columns])
-            nc.sync.dma_start(out=by_lane[b, r, m], in_=result[:])
-
         on_scalar = nc.scalar.copy
         on_vector = nc.vector.tensor_copy
 
@@ -270,50 +257,61 @@ def tile_bilinearpairedlayer_pa_kernel(tc, x_l, W_l_words, W_l_scales, b_l, W_bi
             quantise(grouped, h_codes, h_scales, c, slice(b * POS, (b + 1) * POS))
 
         h_00 = hidden_planes(0, 0)
-        v_000 = regroup(v_half(0, 0, 0), "v_grouped")
-        v_001 = regroup(v_half(0, 0, 1), "v_grouped")
+        v_000 = regroup(v_raw[0, 0, 0], "v_grouped")
+        split_words(1, slice(0, 2))
         quantise_v(v_000, 0, 0, 0)
+        flipped_10 = flip(1, 0)
+        flipped_11 = flip(1, 1)
+        place(1, 0, flipped_10, nc.scalar.copy)
+        place(1, 1, flipped_11, nc.scalar.copy)
+        v_001 = regroup(v_raw[0, 0, 1], "v_grouped")
         hg_00 = regroup(h_00[:], "h_grouped")
         quantise_v(v_001, 0, 0, 1)
-        h_01 = hidden_planes(0, 1)
-        v_010 = regroup(v_half(0, 1, 0), "v_grouped")
+        quantise_x(1, slice(P, 5 * P))
         quantise_h(hg_00, 0, 0)
+        quantise_x(1, slice(0, P))
+        quantise_x(1, slice(5 * P, 6 * P))
+        h_01 = hidden_planes(0, 1)
+        v_010 = regroup(v_raw[0, 1, 0], "v_grouped")
         hg_01 = regroup(h_01[:], "h_grouped")
         quantise_v(v_010, 0, 1, 0)
-        v_011 = regroup(v_half(0, 1, 1), "v_grouped")
+        v_011 = regroup(v_raw[0, 1, 1], "v_grouped")
         quantise_h(hg_01, 0, 1)
         h_10 = hidden_planes(1, 0)
-        hg_10 = regroup(h_10[:], "h_grouped")
+        v_100 = regroup(v_raw[1, 0, 0], "v_grouped")
         quantise_v(v_011, 0, 1, 1)
-        v_100 = regroup(v_half(1, 0, 0), "v_grouped")
-        quantise_h(hg_10, 1, 0)
+        v_110 = regroup(v_raw[1, 1, 0], "v_grouped")
+        quantise_v(v_100, 1, 0, 0)
+
         h_11 = stage.tile([P, PACK, POS], BF16, name="h_planes")
         hidden_tile(1, 1, 0, h_11)
         hidden_tile(1, 1, 1, h_11)
-        store_lane(0, 0, 0, (on_scalar, on_scalar))
-        hidden_tile(1, 1, 2, h_11)
-        store_lane(0, 0, 1, (on_scalar, on_scalar))
-        hidden_tile(1, 1, 3, h_11)
-        store_lane(0, 0, 2, (on_scalar, on_scalar))
-        store_lane(0, 0, 3, (on_scalar, on_scalar))
-        v_110 = regroup(v_half(1, 1, 0), "v_grouped")
-        quantise_v(v_100, 1, 0, 0)
+        for r in range(LANES):
+            store_half(0, 0, 0, r, on_scalar)
+            if r % 2 == 1:
+                hidden_tile(1, 1, 2 + r // 2, h_11)
+        hg_10 = regroup(h_10[:], "h_grouped")
         quantise_v(v_110, 1, 1, 0)
         hg_11 = regroup(h_11[:], "h_grouped")
-        v_101 = regroup(v_half(1, 0, 1), "v_grouped")
+        quantise_h(hg_10, 1, 0)
+        v_101 = regroup(v_raw[1, 0, 1], "v_grouped")
         quantise_h(hg_11, 1, 1)
-        v_111 = regroup(v_half(1, 1, 1), "v_grouped")
+        v_111 = regroup(v_raw[1, 1, 1], "v_grouped")
         quantise_v(v_101, 1, 0, 1)
         quantise_v(v_111, 1, 1, 1)
 
         for r in range(LANES):
+            store_half(0, 1, 0, r, on_scalar)
+        for r in range(LANES):
             store_half(1, 0, 0, r, on_scalar)
         for r in range(LANES):
-            store_lane(0, 1, r, (on_scalar, on_vector if r >= 2 else on_scalar))
+            for half in range(HID // BANK):
+                store_half(0, half, 1, r, on_scalar)
         for r in range(LANES):
             store_half(1, 1, 0, r, on_vector if r % 2 == 0 else on_scalar)
         for r in range(LANES - 1):
-            store_lane(1, 1, r, (on_vector, on_scalar))
+            store_half(1, 0, 1, r, on_vector)
+            store_half(1, 1, 1, r, on_scalar)
         store_half(1, 0, 1, LANES - 1, on_vector)
         store_part(1, BANK, BANK // 2, 1, LANES - 1, on_scalar)
         store_part(1, BANK + BANK // 2, BANK // 2, 1, LANES - 1, on_vector)

@@ -39,7 +39,7 @@ def tile_bilinearpairedlayer_pa_kernel(tc, x_l, W_l_words, W_l_scales, b_l, W_bi
         keep = ctx.enter_context(tc.tile_pool(name="keep", bufs=1))
         raw_pool = ctx.enter_context(tc.tile_pool(name="raw", bufs=3))
         stage = ctx.enter_context(tc.tile_pool(name="stage", bufs=3))
-        out_pool = ctx.enter_context(tc.tile_pool(name="outs", bufs=16))
+        out_pool = ctx.enter_context(tc.tile_pool(name="outs", bufs=8))
         psum = ctx.enter_context(tc.psum_pool(name="psum", bufs=8))
 
         ident = keep.tile([P, P], F32)
@@ -241,6 +241,13 @@ def tile_bilinearpairedlayer_pa_kernel(tc, x_l, W_l_words, W_l_scales, b_l, W_bi
         def store_half(m, half, b, r, copy):
             store_part(m, half * BANK, BANK, b, r, copy)
 
+        def store_lane(m, b, r, copies):
+            result = out_pool.tile([P, HID], F32, name="result")
+            for half in range(HID // BANK):
+                columns = slice(half * BANK, (half + 1) * BANK)
+                second_layer(m, columns, b, r, copies[half], result[:, columns])
+            nc.sync.dma_start(out=by_lane[b, r, m], in_=result[:])
+
         on_scalar = nc.scalar.copy
         on_vector = nc.vector.tensor_copy
 
@@ -278,40 +285,28 @@ def tile_bilinearpairedlayer_pa_kernel(tc, x_l, W_l_words, W_l_scales, b_l, W_bi
         v_011 = regroup(v_raw[0, 1, 1], "v_grouped")
         quantise_h(hg_01, 0, 1)
         h_10 = hidden_planes(1, 0)
-        v_100 = regroup(v_raw[1, 0, 0], "v_grouped")
-        quantise_v(v_011, 0, 1, 1)
-        v_110 = regroup(v_raw[1, 1, 0], "v_grouped")
-        quantise_v(v_100, 1, 0, 0)
-
-        h_11 = stage.tile([P, PACK, POS], BF16, name="h_planes")
-        hidden_tile(1, 1, 0, h_11)
-        hidden_tile(1, 1, 1, h_11)
-        for r in range(LANES):
-            store_half(0, 0, 0, r, on_scalar)
-            if r % 2 == 1:
-                hidden_tile(1, 1, 2 + r // 2, h_11)
         hg_10 = regroup(h_10[:], "h_grouped")
-        quantise_v(v_110, 1, 1, 0)
-        hg_11 = regroup(h_11[:], "h_grouped")
+        quantise_v(v_011, 0, 1, 1)
+        h_11 = hidden_planes(1, 1)
+        v_100 = regroup(v_raw[1, 0, 0], "v_grouped")
         quantise_h(hg_10, 1, 0)
-        v_101 = regroup(v_raw[1, 0, 1], "v_grouped")
+        hg_11 = regroup(h_11[:], "h_grouped")
+        quantise_v(v_100, 1, 0, 0)
         quantise_h(hg_11, 1, 1)
+        v_110 = regroup(v_raw[1, 1, 0], "v_grouped")
+        v_101 = regroup(v_raw[1, 0, 1], "v_grouped")
+        quantise_v(v_110, 1, 1, 0)
         v_111 = regroup(v_raw[1, 1, 1], "v_grouped")
         quantise_v(v_101, 1, 0, 1)
         quantise_v(v_111, 1, 1, 1)
 
+        for b in range(SEQS):
+            for r in range(LANES):
+                store_lane(0, b, r, (on_scalar, on_scalar))
         for r in range(LANES):
-            store_half(0, 1, 0, r, on_scalar)
-        for r in range(LANES):
-            store_half(1, 0, 0, r, on_scalar)
-        for r in range(LANES):
-            for half in range(HID // BANK):
-                store_half(0, half, 1, r, on_scalar)
-        for r in range(LANES):
-            store_half(1, 1, 0, r, on_vector if r % 2 == 0 else on_scalar)
+            store_lane(1, 0, r, (on_vector, on_scalar))
         for r in range(LANES - 1):
-            store_half(1, 0, 1, r, on_vector)
-            store_half(1, 1, 1, r, on_scalar)
+            store_lane(1, 1, r, (on_vector, on_scalar))
         store_half(1, 0, 1, LANES - 1, on_vector)
         store_part(1, BANK, BANK // 2, 1, LANES - 1, on_scalar)
         store_part(1, BANK + BANK // 2, BANK // 2, 1, LANES - 1, on_vector)

@@ -47,18 +47,18 @@ def tile_bilinearpairedlayer_pa_kernel(tc, x_l, W_l_words, W_l_scales, b_l, W_bi
         x_rows = keep.tile([P, SEQS, LANES * FEAT], BF16)
         x_halves = keep.tile([P, SEQS, LANES * FEAT // 2], F32)
         x_grouped = keep.tile([P, SEQS, SLOTS * P, PACK], BF16, align_bytes=64)
-        x_codes = keep.tile([P, SEQS, SLOTS * P], U32, align_bytes=64)
-        x_scales = keep.tile([P, SEQS, SLOTS * P], U8, align_bytes=64)
-        w_codes = keep.tile([P, 3, HID], U32, align_bytes=64)
-        w_scales = keep.tile([P, 3, HID], U8, align_bytes=64)
+        x_codes = keep.tile([P, SEQS, SLOTS * P], U32, align_bytes=256)
+        x_scales = keep.tile([P, SEQS, SLOTS * P], U8, align_bytes=256)
+        w_codes = keep.tile([P, 3, HID], U32, align_bytes=256)
+        w_scales = keep.tile([P, 3, HID], U8, align_bytes=256)
         table_probe = keep.tile([P, 2], F32)
         blank = keep.tile([P, BANK], BF16)
         bias_rows = keep.tile([P, P], BF16)
         bias_cols = keep.tile([P, H_TILES], F32)
-        h_codes = keep.tile([P, H_PASSES, TOKENS], U32, align_bytes=64)
-        h_scales = keep.tile([P, H_PASSES, TOKENS], U8, align_bytes=64)
-        v_codes = keep.tile([P, H_PASSES, MAPS * HID], U32, align_bytes=64)
-        v_scales = keep.tile([P, H_PASSES, MAPS * HID], U8, align_bytes=64)
+        h_codes = keep.tile([P, H_PASSES, TOKENS], U32, align_bytes=256)
+        h_scales = keep.tile([P, H_PASSES, TOKENS], U8, align_bytes=256)
+        v_codes = keep.tile([P, H_PASSES, MAPS * HID], U32, align_bytes=256)
+        v_scales = keep.tile([P, H_PASSES, MAPS * HID], U8, align_bytes=256)
 
         x_words = x_rows[:].bitcast(F32)
         x_grouped_words = x_grouped[:].bitcast(F32)

@@ -37,7 +37,6 @@ def tile_bilinearpairedlayer_pa_kernel(tc, x_l, W_l_words, W_l_scales, b_l, W_bi
     with ExitStack() as ctx:
         ctx.enter_context(tc.manual_schedule())
         keep = ctx.enter_context(tc.tile_pool(name="keep", bufs=1))
-        raw_pool = ctx.enter_context(tc.tile_pool(name="raw", bufs=3))
         stage = ctx.enter_context(tc.tile_pool(name="stage", bufs=3))
         out_pool = ctx.enter_context(tc.tile_pool(name="outs", bufs=8))
         psum = ctx.enter_context(tc.psum_pool(name="psum", bufs=8))
@@ -73,10 +72,8 @@ def tile_bilinearpairedlayer_pa_kernel(tc, x_l, W_l_words, W_l_scales, b_l, W_bi
         make_identity(nc, ident_bf16[:])
 
         x_by_lane = x_l.rearrange("b (a r) k -> b a (r k)", r=LANES)
-        for pair in range(LANES // 2):
-            columns = slice(pair * 2 * FEAT, (pair + 1) * 2 * FEAT)
-            nc.sync.dma_start(out=x_rows[:, 0, columns], in_=x_by_lane[0][:, columns])
-        nc.sync.dma_start(out=bias_rows[0:H_TILES, :], in_=b_l.rearrange("(j p) -> j p", p=P))
+        nc.sync.dma_start(out=x_rows[:, 0, :], in_=x_by_lane[0])
+        nc.scalar.dma_start(out=bias_rows[0:H_TILES, :], in_=b_l.rearrange("(j p) -> j p", p=P))
         w_bytes = W_l_words.rearrange("g p n t -> p g (n t)")
 
         def load_w(c):
@@ -87,14 +84,14 @@ def tile_bilinearpairedlayer_pa_kernel(tc, x_l, W_l_words, W_l_scales, b_l, W_bi
 
         v_raw = {}
 
-        def load_v(m, c, halves):
+        def load_v(name, m, passes, halves):
             columns = slice(halves[0] * BANK, (halves[-1] + 1) * BANK)
-            raw = raw_pool.tile([P, PACK, len(halves) * BANK], BF16, name="raw_%d" % len(halves))
-            nc.sync.dma_start(
-                out=raw[:], in_=W_bil[m].rearrange("(c t p) n -> c p t n", t=PACK, p=P)[c][:, :, columns]
-            )
-            for i, half in enumerate(halves):
-                v_raw[m, c, half] = raw[:, :, i * BANK : (i + 1) * BANK]
+            units = slice(passes[0] * K_PASS, (passes[-1] + 1) * K_PASS)
+            raw = keep.tile([P, len(passes) * PACK, len(halves) * BANK], BF16, name=name)
+            nc.sync.dma_start(out=raw[:], in_=W_bil[m][units, columns].rearrange("(t p) n -> p t n", p=P))
+            for i, c in enumerate(passes):
+                for k, half in enumerate(halves):
+                    v_raw[m, c, half] = raw[:, i * PACK : (i + 1) * PACK, k * BANK : (k + 1) * BANK]
 
         load_w(0)
         for quad in range(4):
@@ -102,13 +99,12 @@ def tile_bilinearpairedlayer_pa_kernel(tc, x_l, W_l_words, W_l_scales, b_l, W_bi
                 out=w_scales[32 * quad : 32 * quad + 4, :, :].bitcast(I32),
                 in_=W_l_scales[:, 4 * quad : 4 * quad + 4, :].rearrange("g q n -> q g n").bitcast(I32),
             )
-        load_v(0, 0, (0,))
+        load_v("v_left", 0, (0,), (0,))
         nc.sync.dma_start(out=x_rows[:, 1, :], in_=x_by_lane[1])
-        load_v(0, 0, (1,))
+        load_v("v_right", 0, (0,), (1,))
         load_w(1)
-        load_v(0, 1, (0, 1))
-        load_v(1, 0, (0, 1))
-        load_v(1, 1, (0, 1))
+        load_v("v_second", 0, (1,), (0, 1))
+        load_v("v_map_1", 1, (0, 1), (0, 1))
 
         nc.scalar.activation(out=table_probe[:, 1:2], in_=table_probe[:, 0:1], func=RELU)
 

@@ -62,7 +62,7 @@ def tile_bilinearpairedlayer_pa_kernel(tc, x_l, W_l_words, W_l_scales, b_l, W_bi
         x_words = x_rows[:].bitcast(F32)
         x_grouped_words = x_grouped[:].bitcast(F32)
 
-        nc.vector.memset(blank[:], 0.0)
+        nc.vector.memset(blank[:].bitcast(I32), 0)
         nc.vector.memset(bias_rows[:], 0.0)
         nc.vector.memset(table_probe[:], 0.0)
         nc.vector.memset(w_scales[:].bitcast(I32), 0)
@@ -101,8 +101,8 @@ def tile_bilinearpairedlayer_pa_kernel(tc, x_l, W_l_words, W_l_scales, b_l, W_bi
             )
         load_v("v_left", 0, (0,), (0,))
         nc.sync.dma_start(out=x_rows[:, 1, :], in_=x_by_lane[1])
-        load_v("v_right", 0, (0,), (1,))
         load_w(1)
+        load_v("v_right", 0, (0,), (1,))
         load_v("v_second", 0, (1,), (0, 1))
         load_v("v_map_1", 1, (0, 1), (0, 1))
 
@@ -132,20 +132,21 @@ def tile_bilinearpairedlayer_pa_kernel(tc, x_l, W_l_words, W_l_scales, b_l, W_bi
                     )
             return flipped
 
-        def place(b, pair, flipped, copy):
+        def place(b, pair, flipped, copy, copy_shifted):
             columns = slice((1 + 2 * pair) * P, (3 + 2 * pair) * P)
-            target = x_grouped_words[:, b, columns, :].rearrange("p (s a) u -> p s a u", s=2)
-            source = flipped[:].rearrange("p s u a -> p s a u")
+            copy(
+                out=x_grouped_words[:, b, columns, :].rearrange("p (s a) u -> p s a u", s=2),
+                in_=flipped[:].rearrange("p s u a -> p s a u"),
+            )
             if pair == 0:
-                copy(out=target, in_=source)
-                copy(
+                copy_shifted(
                     out=x_grouped_words[:, b, (LANES + 1) * P : SLOTS * P - 1, :],
                     in_=flipped[:, 0, :, 1:P].rearrange("p u a -> p a u"),
                 )
             else:
-                copy(out=target, in_=source)
-                copy(
-                    out=x_grouped_words[:, b, 1:P, :], in_=flipped[:, 1, :, 0 : P - 1].rearrange("p u a -> p a u")
+                copy_shifted(
+                    out=x_grouped_words[:, b, 1:P, :],
+                    in_=flipped[:, 1, :, 0 : P - 1].rearrange("p u a -> p a u"),
                 )
 
         def quantise_x(b, columns):
@@ -155,18 +156,34 @@ def tile_bilinearpairedlayer_pa_kernel(tc, x_l, W_l_words, W_l_scales, b_l, W_bi
                 in_=x_grouped[:, b, columns, :].rearrange("p c t -> p (c t)"),
             )
 
-        keep_busy(4)
+        def flip_lane(lane):
+            flipped = psum.tile([P, 2, P], F32, tag="bank", name="flipped_lane")
+            for u in range(2):
+                first = (2 * lane + u) * P
+                nc.tensor.transpose(out=flipped[:, u, :], in_=x_halves[:, 0, first : first + P], identity=ident[:])
+            return flipped
+
+        def place_lane(slot, source, copy, rows=slice(0, P)):
+            copy(
+                out=x_grouped_words[:, 0, slot * P + rows.start : slot * P + rows.stop, :],
+                in_=source.rearrange("p u a -> p a u"),
+            )
+
+        keep_busy(5)
         split_words(0, slice(0, 1))
         split_words(0, slice(1, 2))
-        flipped_00 = flip(0, 0)
-        flipped_01 = flip(0, 1)
+        lanes = []
+        for lane in range(LANES):
+            lanes.append(flip_lane(lane))
 
         bias_flipped = psum.tile([P, P], BF16, tag="bank", name="bias_flipped")
         nc.tensor.transpose(out=bias_flipped[:], in_=bias_rows[:], identity=ident_bf16[:])
         keep_busy(3)
 
-        place(0, 0, flipped_00, nc.vector.tensor_copy)
-        place(0, 1, flipped_01, nc.scalar.copy)
+        for lane in range(LANES):
+            place_lane(lane + 1, lanes[lane][:], nc.vector.tensor_copy if lane % 2 == 0 else nc.scalar.copy)
+        place_lane(0, lanes[3][:, :, 0 : P - 1], nc.scalar.copy, slice(1, P))
+        place_lane(LANES + 1, lanes[0][:, :, 1:P], nc.scalar.copy, slice(0, P - 1))
         nc.scalar.copy(out=bias_cols[:], in_=bias_flipped[:, 0:H_TILES])
         quantise_x(0, slice(P, 3 * P))
         quantise_x(0, slice(3 * P, 5 * P))
@@ -265,20 +282,27 @@ def tile_bilinearpairedlayer_pa_kernel(tc, x_l, W_l_words, W_l_scales, b_l, W_bi
         quantise_v(v_000, 0, 0, 0)
         flipped_10 = flip(1, 0)
         flipped_11 = flip(1, 1)
-        place(1, 0, flipped_10, nc.scalar.copy)
-        place(1, 1, flipped_11, nc.scalar.copy)
-        v_001 = regroup(v_raw[0, 0, 1], "v_grouped")
+        place(1, 0, flipped_10, nc.vector.tensor_copy, nc.scalar.copy)
+        place(1, 1, flipped_11, nc.scalar.copy, nc.scalar.copy)
         hg_00 = regroup(h_00[:], "h_grouped")
-        quantise_v(v_001, 0, 0, 1)
         quantise_x(1, slice(P, 5 * P))
         quantise_h(hg_00, 0, 0)
         quantise_x(1, slice(0, P))
         quantise_x(1, slice(5 * P, 6 * P))
-        h_01 = hidden_planes(0, 1)
+        v_001 = stage.tile([P, BANK, PACK], BF16, align_bytes=64, name="v_by_scalar")
+        h_01 = stage.tile([P, PACK, POS], BF16, name="h_planes")
+        for t in range(PACK):
+            hidden_tile(0, 1, t, h_01)
+            columns = slice(t * P, (t + 1) * P)
+            nc.scalar.copy(
+                out=v_001[:, columns, :].rearrange("p (c i) t -> p c t i", i=4),
+                in_=v_raw[0, 0, 1][:, :, columns].rearrange("p t (c i) -> p c t i", i=4),
+            )
         v_010 = regroup(v_raw[0, 1, 0], "v_grouped")
-        hg_01 = regroup(h_01[:], "h_grouped")
-        quantise_v(v_010, 0, 1, 0)
         v_011 = regroup(v_raw[0, 1, 1], "v_grouped")
+        quantise_v(v_010, 0, 1, 0)
+        hg_01 = regroup(h_01[:], "h_grouped")
+        quantise_v(v_001, 0, 0, 1)
         quantise_h(hg_01, 0, 1)
         h_10 = hidden_planes(1, 0)
         hg_10 = regroup(h_10[:], "h_grouped")

@@ -254,12 +254,20 @@ def tile_bilinearpairedlayer_pa_kernel(tc, x_l, W_l_words, W_l_scales, b_l, W_bi
         def store_half(m, half, b, r, copy):
             store_part(m, half * BANK, BANK, b, r, copy)
 
+        for_scalar = []
+
         def store_lane(m, b, r, copies):
             result = out_pool.tile([P, HID], F32, name="result")
             for half in range(HID // BANK):
                 columns = slice(half * BANK, (half + 1) * BANK)
                 second_layer(m, columns, b, r, copies[half], result[:, columns])
-            nc.sync.dma_start(out=by_lane[b, r, m], in_=result[:])
+                while for_scalar:
+                    target, source = for_scalar.pop()
+                    nc.scalar.dma_start(out=target, in_=source)
+            if r % 2 == 0:
+                nc.sync.dma_start(out=by_lane[b, r, m], in_=result[:])
+            else:
+                for_scalar.append((by_lane[b, r, m], result[:]))
 
         on_scalar = nc.scalar.copy
         on_vector = nc.vector.tensor_copy

@@ -94,11 +94,9 @@ def tile_bilinearpairedlayer_pa_kernel(tc, x_l, W_l_words, W_l_scales, b_l, W_bi
                     v_raw[m, c, half] = raw[:, i * PACK : (i + 1) * PACK, k * BANK : (k + 1) * BANK]
 
         load_w(0)
-        for quad in range(4):
-            nc.sync.dma_start(
-                out=w_scales[32 * quad : 32 * quad + 4, :, :].bitcast(I32),
-                in_=W_l_scales[:, 4 * quad : 4 * quad + 4, :].rearrange("g q n -> q g n").bitcast(I32),
-            )
+        scale_rows = W_l_scales.rearrange("g (quad row) n -> row quad g n", row=4)
+        for row in range(4):
+            nc.sync.dma_start(out=w_scales[row:P:32, :, :].bitcast(I32), in_=scale_rows[row].bitcast(I32))
         load_v("v_left", 0, (0,), (0,))
         nc.sync.dma_start(out=x_rows[:, 1, :], in_=x_by_lane[1])
         load_w(1)

@@ -219,7 +219,11 @@ def tile_bilinearpairedlayer_pa_kernel(tc, x_l, W_l_words, W_l_scales, b_l, W_bi
                     stop=(g == 2),
                 )
             nc.scalar.activation(
-                out=h_planes[:, t, :], in_=pre[:], func=RELU, bias=bias_cols[:, j : j + 1], scale=1.0
+                out=h_planes[:, t, :].rearrange("p (a r) -> p a r", r=LANES),
+                in_=pre[:].rearrange("p (r a) -> p a r", r=LANES),
+                func=RELU,
+                bias=bias_cols[:, j : j + 1],
+                scale=1.0,
             )
 
         def map_columns(m, half):
@@ -241,7 +245,7 @@ def tile_bilinearpairedlayer_pa_kernel(tc, x_l, W_l_words, W_l_scales, b_l, W_bi
                 )
             copy(out=target, in_=acc[:])
 
-        by_lane = out.rearrange("b (a r) m g -> b r m a g", r=LANES)
+        by_lane = out.rearrange("b (r a) m g -> b r m a g", r=LANES)
 
         def store_part(m, first, width, b, r, copy):
             result = out_pool.tile([P, width], F32, name="part_%d" % width)

from contextlib import ExitStack

import concourse.mybir as mybir
from concourse.masks import make_identity

F32 = mybir.dt.float32
BF16 = mybir.dt.bfloat16
I32 = mybir.dt.int32
U32 = mybir.dt.uint32
U8 = mybir.dt.uint8
FP8X4 = mybir.dt.float8_e4m3fn_x4
RELU = mybir.ActivationFunctionType.Relu

P = 128
PACK = 4
K_PASS = P * PACK
BANK = 512

SEQS = 2
POS = 512
FEAT = 512
HID = 1024
MAPS = 2
TOKENS = SEQS * POS

LANES = POS // P
SLOTS = LANES + 2
SHIFT_OF_GROUP = (0, -1, 1)
H_TILES = HID // P
H_PASSES = HID // K_PASS

FLOPS = 2 * TOKENS * (3 * FEAT) * HID + 2 * TOKENS * HID * (MAPS * HID)


def tile_bilinearpairedlayer_pa_kernel(tc, x_l, W_l_words, W_l_scales, b_l, W_bil, out):
    nc = tc.nc
    with ExitStack() as ctx:
        ctx.enter_context(tc.manual_schedule())
        keep = ctx.enter_context(tc.tile_pool(name="keep", bufs=1))
        stage = ctx.enter_context(tc.tile_pool(name="stage", bufs=3))
        out_pool = ctx.enter_context(tc.tile_pool(name="outs", bufs=8))
        psum = ctx.enter_context(tc.psum_pool(name="psum", bufs=8))

        ident = keep.tile([P, P], F32)
        ident_bf16 = keep.tile([P, P], BF16)
        x_rows = keep.tile([P, SEQS, LANES * FEAT], BF16)
        x_halves = keep.tile([P, SEQS, LANES * FEAT // 2], F32)
        x_grouped = keep.tile([P, SEQS, SLOTS * P, PACK], BF16, align_bytes=64)
        x_codes = keep.tile([P, SEQS, SLOTS * P], U32, align_bytes=256)
        x_scales = keep.tile([P, SEQS, SLOTS * P], U8, align_bytes=256)
        w_codes = keep.tile([P, 3, HID], U32, align_bytes=256)
        w_scales = keep.tile([P, 3, HID], U8, align_bytes=256)
        table_probe = keep.tile([P, 2], F32)
        blank = keep.tile([P, BANK], BF16)
        bias_rows = keep.tile([P, P], BF16)
        bias_cols = keep.tile([P, H_TILES], F32)
        h_codes = keep.tile([P, H_PASSES, TOKENS], U32, align_bytes=256)
        h_scales = keep.tile([P, H_PASSES, TOKENS], U8, align_bytes=256)
        v_codes = keep.tile([P, H_PASSES, MAPS * HID], U32, align_bytes=256)
        v_scales = keep.tile([P, H_PASSES, MAPS * HID], U8, align_bytes=256)

        x_words = x_rows[:].bitcast(F32)
        x_grouped_words = x_grouped[:].bitcast(F32)

        nc.vector.memset(blank[:].bitcast(I32), 0)
        nc.vector.memset(bias_rows[:], 0.0)
        nc.vector.memset(table_probe[:], 0.0)
        nc.vector.memset(w_scales[:].bitcast(I32), 0)
        nc.vector.memset(x_grouped_words[:, :, 0:4, :], 0.0)
        nc.vector.memset(x_grouped_words[:, :, SLOTS * P - 4 : SLOTS * P, :], 0.0)
        make_identity(nc, ident[:])
        make_identity(nc, ident_bf16[:])

        x_by_lane = x_l.rearrange("b (a r) k -> b a (r k)", r=LANES)
        nc.sync.dma_start(out=x_rows[:, 0, :], in_=x_by_lane[0])
        nc.scalar.dma_start(out=bias_rows[0:H_TILES, :], in_=b_l.rearrange("(j p) -> j p", p=P))
        w_bytes = W_l_words.rearrange("g p n t -> p g (n t)")

        def load_w(c):
            nc.sync.dma_start(
                out=w_codes[:, :, c * K_PASS : (c + 1) * K_PASS].bitcast(I32),
                in_=w_bytes[:, :, c * K_PASS * PACK : (c + 1) * K_PASS * PACK].bitcast(I32),
            )

        v_raw = {}

        def load_v(name, m, passes, halves):
            columns = slice(halves[0] * BANK, (halves[-1] + 1) * BANK)
            units = slice(passes[0] * K_PASS, (passes[-1] + 1) * K_PASS)
            raw = keep.tile([P, len(passes) * PACK, len(halves) * BANK], BF16, name=name)
            nc.sync.dma_start(out=raw[:], in_=W_bil[m][units, columns].rearrange("(t p) n -> p t n", p=P))
            for i, c in enumerate(passes):
                for k, half in enumerate(halves):
                    v_raw[m, c, half] = raw[:, i * PACK : (i + 1) * PACK, k * BANK : (k + 1) * BANK]

        load_w(0)
        scale_rows = W_l_scales.rearrange("g (quad row) n -> row quad g n", row=4)
        for row in range(4):
            nc.sync.dma_start(out=w_scales[row:P:32, :, :].bitcast(I32), in_=scale_rows[row].bitcast(I32))
        load_v("v_left", 0, (0,), (0,))
        nc.sync.dma_start(out=x_rows[:, 1, :], in_=x_by_lane[1])
        load_w(1)
        load_v("v_right", 0, (0,), (1,))
        load_v("v_second", 0, (1,), (0, 1))
        load_v("v_map_1", 1, (0, 1), (0, 1))

        nc.scalar.activation(out=table_probe[:, 1:2], in_=table_probe[:, 0:1], func=RELU)

        def keep_busy(count):
            for step in range(count):
                idle = psum.tile([P, BANK], F32, tag="bank", name="idle")
                nc.tensor.matmul(out=idle[:], lhsT=blank[:, 0:P], rhs=blank[:], start=True, stop=True)

        def split_words(b, pairs):
            words = slice(pairs.start * FEAT, pairs.stop * FEAT)
            nc.vector.tensor_copy(
                out=x_halves[:, b, words].rearrange("a (r u p) -> a r u p", u=2, p=P),
                in_=x_words[:, b, words].rearrange("a (r p u) -> a r u p", u=2, p=P),
            )

        def flip(b, pair):
            flipped = psum.tile([P, 2, 2, P], F32, tag="bank", name="flipped")
            for s in range(2):
                first = (2 * pair + s) * 2 * P
                for u in range(2):
                    nc.tensor.transpose(
                        out=flipped[:, s, u, :],
                        in_=x_halves[:, b, first + u * P : first + (u + 1) * P],
                        identity=ident[:],
                    )
            return flipped

        def place(b, pair, flipped, copy, copy_shifted):
            columns = slice((1 + 2 * pair) * P, (3 + 2 * pair) * P)
            copy(
                out=x_grouped_words[:, b, columns, :].rearrange("p (s a) u -> p s a u", s=2),
                in_=flipped[:].rearrange("p s u a -> p s a u"),
            )
            if pair == 0:
                copy_shifted(
                    out=x_grouped_words[:, b, (LANES + 1) * P : SLOTS * P - 1, :],
                    in_=flipped[:, 0, :, 1:P].rearrange("p u a -> p a u"),
                )
            else:
                copy_shifted(
                    out=x_grouped_words[:, b, 1:P, :],
                    in_=flipped[:, 1, :, 0 : P - 1].rearrange("p u a -> p a u"),
                )

        def quantise_x(b, columns):
            nc.vector.quantize_mx(
                out=x_codes[:, b, columns].bitcast(FP8X4),
                scales=x_scales[:, b, columns],
                in_=x_grouped[:, b, columns, :].rearrange("p c t -> p (c t)"),
            )

        def flip_lane(lane):
            flipped = psum.tile([P, 2, P], F32, tag="bank", name="flipped_lane")
            for u in range(2):
                first = (2 * lane + u) * P
                nc.tensor.transpose(out=flipped[:, u, :], in_=x_halves[:, 0, first : first + P], identity=ident[:])
            return flipped

        def place_lane(slot, source, copy, rows=slice(0, P)):
            copy(
                out=x_grouped_words[:, 0, slot * P + rows.start : slot * P + rows.stop, :],
                in_=source.rearrange("p u a -> p a u"),
            )

        keep_busy(5)
        split_words(0, slice(0, 1))
        split_words(0, slice(1, 2))
        lanes = []
        for lane in range(LANES):
            lanes.append(flip_lane(lane))

        bias_flipped = psum.tile([P, P], BF16, tag="bank", name="bias_flipped")
        nc.tensor.transpose(out=bias_flipped[:], in_=bias_rows[:], identity=ident_bf16[:])
        keep_busy(3)

        for lane in range(LANES):
            place_lane(lane + 1, lanes[lane][:], nc.vector.tensor_copy if lane % 2 == 0 else nc.scalar.copy)
        place_lane(0, lanes[3][:, :, 0 : P - 1], nc.scalar.copy, slice(1, P))
        place_lane(LANES + 1, lanes[0][:, :, 1:P], nc.scalar.copy, slice(0, P - 1))
        nc.scalar.copy(out=bias_cols[:], in_=bias_flipped[:, 0:H_TILES])
        quantise_x(0, slice(P, 3 * P))
        quantise_x(0, slice(3 * P, 5 * P))
        quantise_x(0, slice(0, P))
        quantise_x(0, slice(5 * P, 6 * P))

        def regroup(planes, name):
            grouped = stage.tile([P, BANK, PACK], BF16, align_bytes=64, name=name)
            nc.vector.tensor_copy(
                out=grouped[:].rearrange("p (c i) t -> p c t i", i=4),
                in_=planes.rearrange("p t (c i) -> p c t i", i=4),
            )
            return grouped

        def quantise(grouped, codes, scales, c, columns):
            nc.vector.quantize_mx(
                out=codes[:, c, columns].bitcast(FP8X4),
                scales=scales[:, c, columns],
                in_=grouped[:].rearrange("p c t -> p (c t)"),
            )

        def hidden_tile(b, c, t, h_planes):
            j = PACK * c + t
            units = slice(j * P, (j + 1) * P)
            pre = psum.tile([P, POS], F32, tag="bank", name="pre")
            for g in range(3):
                first = (1 + SHIFT_OF_GROUP[g]) * P
                nc.tensor.matmul_mx(
                    out=pre[:],
                    lhsT=w_codes[:, g, units].bitcast(FP8X4),
                    lhsT_scale=w_scales[:, g, units],
                    rhs=x_codes[:, b, first : first + POS].bitcast(FP8X4),
                    rhs_scale=x_scales[:, b, first : first + POS],
                    start=(g == 0),
                    stop=(g == 2),
                )
            nc.scalar.activation(
                out=h_planes[:, t, :].rearrange("p (a r) -> p a r", r=LANES),
                in_=pre[:].rearrange("p (r a) -> p a r", r=LANES),
                func=RELU,
                bias=bias_cols[:, j : j + 1],
                scale=1.0,
            )

        def map_columns(m, half):
            return slice(m * HID + half * BANK, m * HID + (half + 1) * BANK)

        def second_layer(m, columns, b, r, copy, target):
            tokens = slice(b * POS + r * P, b * POS + (r + 1) * P)
            of_maps = slice(m * HID + columns.start, m * HID + columns.stop)
            acc = psum.tile([P, columns.stop - columns.start], F32, tag="bank", name="acc")
            for c in range(H_PASSES):
                nc.tensor.matmul_mx(
                    out=acc[:],
                    lhsT=h_codes[:, c, tokens].bitcast(FP8X4),
                    lhsT_scale=h_scales[:, c, tokens],
                    rhs=v_codes[:, c, of_maps].bitcast(FP8X4),
                    rhs_scale=v_scales[:, c, of_maps],
                    start=(c == 0),
                    stop=(c == H_PASSES - 1),
                )
            copy(out=target, in_=acc[:])

        by_lane = out.rearrange("b (r a) m g -> b r m a g", r=LANES)

        def store_part(m, first, width, b, r, copy):
            result = out_pool.tile([P, width], F32, name="part_%d" % width)
            columns = slice(first, first + width)
            second_layer(m, columns, b, r, copy, result[:])
            nc.sync.dma_start(out=by_lane[b, r, m][:, columns], in_=result[:])

        def store_half(m, half, b, r, copy):
            store_part(m, half * BANK, BANK, b, r, copy)

        for_scalar = []

        def store_lane(m, b, r, copies):
            result = out_pool.tile([P, HID], F32, name="result")
            for half in range(HID // BANK):
                columns = slice(half * BANK, (half + 1) * BANK)
                second_layer(m, columns, b, r, copies[half], result[:, columns])
                while for_scalar:
                    target, source = for_scalar.pop()
                    nc.scalar.dma_start(out=target, in_=source)
            if r % 2 == 0:
                nc.sync.dma_start(out=by_lane[b, r, m], in_=result[:])
            else:
                for_scalar.append((by_lane[b, r, m], result[:]))

        on_scalar = nc.scalar.copy
        on_vector = nc.vector.tensor_copy

        def hidden_planes(b, c):
            h_planes = stage.tile([P, PACK, POS], BF16, name="h_planes")
            for t in range(PACK):
                hidden_tile(b, c, t, h_planes)
            return h_planes

        def quantise_v(grouped, m, c, half):
            quantise(grouped, v_codes, v_scales, c, map_columns(m, half))

        def quantise_h(grouped, b, c):
            quantise(grouped, h_codes, h_scales, c, slice(b * POS, (b + 1) * POS))

        h_00 = hidden_planes(0, 0)
        v_000 = regroup(v_raw[0, 0, 0], "v_grouped")
        split_words(1, slice(0, 2))
        quantise_v(v_000, 0, 0, 0)
        flipped_10 = flip(1, 0)
        flipped_11 = flip(1, 1)
        place(1, 0, flipped_10, nc.vector.tensor_copy, nc.scalar.copy)
        place(1, 1, flipped_11, nc.scalar.copy, nc.scalar.copy)
        hg_00 = regroup(h_00[:], "h_grouped")
        quantise_x(1, slice(P, 5 * P))
        quantise_h(hg_00, 0, 0)
        quantise_x(1, slice(0, P))
        quantise_x(1, slice(5 * P, 6 * P))
        v_001 = stage.tile([P, BANK, PACK], BF16, align_bytes=64, name="v_by_scalar")
        h_01 = stage.tile([P, PACK, POS], BF16, name="h_planes")
        for t in range(PACK):
            hidden_tile(0, 1, t, h_01)
            columns = slice(t * P, (t + 1) * P)
            nc.scalar.copy(
                out=v_001[:, columns, :].rearrange("p (c i) t -> p c t i", i=4),
                in_=v_raw[0, 0, 1][:, :, columns].rearrange("p t (c i) -> p c t i", i=4),
            )
        v_010 = regroup(v_raw[0, 1, 0], "v_grouped")
        v_011 = regroup(v_raw[0, 1, 1], "v_grouped")
        quantise_v(v_010, 0, 1, 0)
        hg_01 = regroup(h_01[:], "h_grouped")
        quantise_v(v_001, 0, 0, 1)
        quantise_h(hg_01, 0, 1)
        h_10 = hidden_planes(1, 0)
        hg_10 = regroup(h_10[:], "h_grouped")
        quantise_v(v_011, 0, 1, 1)
        h_11 = hidden_planes(1, 1)
        v_100 = regroup(v_raw[1, 0, 0], "v_grouped")
        quantise_h(hg_10, 1, 0)
        hg_11 = regroup(h_11[:], "h_grouped")
        quantise_v(v_100, 1, 0, 0)
        quantise_h(hg_11, 1, 1)
        v_110 = regroup(v_raw[1, 1, 0], "v_grouped")
        v_101 = regroup(v_raw[1, 0, 1], "v_grouped")
        quantise_v(v_110, 1, 1, 0)
        v_111 = regroup(v_raw[1, 1, 1], "v_grouped")
        quantise_v(v_101, 1, 0, 1)
        quantise_v(v_111, 1, 1, 1)

        for b in range(SEQS):
            for r in range(LANES):
                store_lane(0, b, r, (on_scalar, on_scalar))
        for r in range(LANES):
            store_lane(1, 0, r, (on_vector, on_scalar))
        for r in range(LANES - 1):
            store_lane(1, 1, r, (on_vector, on_scalar))
        store_half(1, 0, 1, LANES - 1, on_vector)
        store_part(1, BANK, BANK // 2, 1, LANES - 1, on_scalar)
        store_part(1, BANK + BANK // 2, BANK // 2, 1, LANES - 1, on_vector)
